import numpy as np
import ml_dtypes


def mxq(x, axis, fmt="e4m3"):
    dtype, down = {"e4m3": (ml_dtypes.float8_e4m3fn, 7), "e5m2": (ml_dtypes.float8_e5m2, 14)}[fmt]
    v = np.moveaxis(np.asarray(x, np.float32).astype(ml_dtypes.bfloat16).astype(np.float64), axis, -1)
    blocks = v.reshape(v.shape[:-1] + (-1, 32))
    amax = np.abs(blocks).max(-1, keepdims=True)
    byte = np.maximum(np.where(amax > 0, np.frexp(amax)[1] - 1 + 127, 0) - down, 1)
    scale = np.exp2(byte - 127.0)
    codes = (blocks / scale).astype(np.float32).astype(dtype).astype(np.float64)
    return np.moveaxis((codes * scale).reshape(v.shape), -1, axis)


WIDE = False


def mx_kscale(k):
    if not WIDE:
        return np.ones(k)
    levels = np.array([10, -10, 5, -5, 0])
    a = np.random.permutation(np.resize(levels, k // 512 * 4)).reshape(k // 512, 4)
    idx = np.arange(k)
    return np.exp2(a[idx // 512, idx % 128 // 32])


BF16 = ml_dtypes.bfloat16


def bf(x):
    return np.asarray(x, np.float32).astype(BF16)


def f64(x):
    return np.asarray(x).astype(np.float64)


B, S, D, NH, NKV, HD, QB = 1, 512, 2048, 16, 4, 128, 512
Q_DIM = NH * HD
N_REP = NH // NKV
NEG = -1.0e30


def setup_inputs():
    t = mx_kscale(Q_DIM).reshape(NKV, N_REP, HD)[:, :1, :]
    tq = np.broadcast_to(t, (NKV, N_REP, HD)).reshape(Q_DIM)
    v_mean = np.where(np.random.standard_normal((B, NKV, 1, HD)) < 0.0, -1.0, 1.0)
    return {"q_rot": bf(np.random.standard_normal((B, NH, S, HD)) * np.sqrt(2.0)),
            "k_rot": bf(np.random.standard_normal((B, NKV, S, HD)) * np.sqrt(2.0)),
            "v": bf((v_mean + np.random.standard_normal((B, NKV, S, HD)) * 0.75) * t),
            "Wo": bf(np.random.standard_normal((D, Q_DIM)) / np.sqrt(Q_DIM) / tq)}


def reference(q_rot, k_rot, v, Wo):
    q5 = f64(q_rot).reshape(B, NKV, N_REP, S, HD)
    kt = f64(k_rot).reshape(B, NKV, 1, S, HD).transpose(0, 1, 2, 4, 3)
    vq = mxq(f64(v).reshape(B, NKV, 1, S, HD), 3, "e4m3")
    pos = np.arange(S)
    blocks = []
    for lo in range(0, S, QB):
        hi = lo + QB
        sc = (q5[:, :, :, lo:hi, :] @ kt[:, :, :, :, :hi]) * (1.0 / np.sqrt(HD))
        sc = np.where(pos[lo:hi, None] >= pos[None, :hi], sc, NEG)
        e = np.exp(sc - sc.max(-1, keepdims=True))
        blocks.append((mxq(e, 4, "e4m3") @ vq[:, :, :, :hi, :]) / e.sum(-1, keepdims=True))
    o = np.concatenate(blocks, axis=3).reshape(B, NH, S, HD).transpose(0, 2, 1, 3).reshape(B, S, Q_DIM)
    return mxq(o, 2, "e4m3") @ mxq(f64(Wo), 1, "e4m3").T

@@ -1,0 +1,422 @@
+from contextlib import ExitStack
+import math
+
+import concourse.mybir as mybir
+from concourse.masks import make_identity
+
+BF16 = mybir.dt.bfloat16
+F32 = mybir.dt.float32
+U32 = mybir.dt.uint32
+U8 = mybir.dt.uint8
+FP8X4 = mybir.dt.float8_e4m3fn_x4
+ACT = mybir.ActivationFunctionType
+ALU = mybir.AluOpType
+AXIS = mybir.AxisListType
+
+P = 128
+S = 512
+HD = 128
+NH = 16
+NKV = 4
+REP = NH // NKV
+D = 2048
+QT = S // P
+K_PASS = 512
+PASSES = D // K_PASS
+N_TILE = 512
+NT = D // N_TILE
+BANK = 512
+SCALE = 1.0 / math.sqrt(HD)
+NEG = -1.0e30
+
+UNITS = QT * NKV
+BEATS = UNITS * REP
+WO_BANKS = 2 * NT * PASSES
+WO_FIRST_BEAT = 8
+DRAIN = 9
+
+FLOPS = 2 * NH * S * S * HD * 2 + 2 * S * D * D
+
+
+def tile_rlaattention_pb_kernel(tc, q_rot, k_rot, v, Wo, out):
+    nc = tc.nc
+    with ExitStack() as ctx:
+        const = ctx.enter_context(tc.tile_pool(name="const", bufs=1))
+        keep = ctx.enter_context(tc.tile_pool(name="keep", bufs=1))
+        work = ctx.enter_context(tc.tile_pool(name="work", bufs=3))
+        stat = ctx.enter_context(tc.tile_pool(name="stat", bufs=6))
+        psum = ctx.enter_context(tc.psum_pool(name="psum", bufs=4))
+        ctx.enter_context(tc.manual_schedule())
+
+        k_sb = keep.tile([P, NKV, QT, HD], BF16)
+        q_sb = keep.tile([P, QT, NH, HD], BF16)
+        v_sb = keep.tile([P, NKV, 4, HD], BF16)
+        wo_sb = keep.tile([P, D // P, D], BF16)
+
+        def load_q(i, h0, h1):
+            nc.sync.dma_start(
+                out=q_sb[:, i, h0:h1, :], in_=q_rot[0, h0:h1, i * P : (i + 1) * P, :].rearrange("h p d -> p h d")
+            )
+
+        def load_wo(c):
+            nc.sync.dma_start(
+                out=wo_sb[:, 2 * c : 2 * c + 2, :],
+                in_=Wo[256 * c : 256 * (c + 1), :].rearrange("(b p) k -> p b k", p=P),
+            )
+
+        for g in range(NKV):
+            nc.sync.dma_start(out=k_sb[:, g], in_=k_rot[0, g].rearrange("(t p) d -> p t d", p=P))
+            load_q(0, g * REP, (g + 1) * REP)
+        nc.sync.dma_start(
+            out=v_sb[:].rearrange("p g (u e) d -> p (g u) (e d)", u=2),
+            in_=v[0].rearrange("g (u p e) d -> p (g u) (e d)", u=2, p=P, e=2),
+        )
+        load_wo(0)
+        load_wo(1)
+        load_q(1, 0, NH)
+        for c in range(2, 6):
+            load_wo(c)
+        load_q(2, 0, NH)
+        load_wo(6)
+        load_wo(7)
+        load_q(3, 0, NH)
+
+        ident_bf = const.tile([P, P], BF16)
+        make_identity(nc, ident_bf[:])
+        ident_f32 = const.tile([P, P], F32)
+        make_identity(nc, ident_f32[:])
+        mask_f32 = const.tile([P, P], F32)
+        nc.gpsimd.memset(mask_f32[:], 0.0)
+        nc.gpsimd.affine_select(
+            out=mask_f32[:],
+            in_=mask_f32[:],
+            pattern=[[-1, P]],
+            compare_op=ALU.is_ge,
+            fill=NEG,
+            base=0,
+            channel_multiplier=1,
+        )
+
+        e_tiles = [keep.tile([P, S], BF16, name="e%d" % slot) for slot in range(2 * REP)]
+        for e_tile in e_tiles:
+            nc.vector.memset(e_tile[:], 0.0)
+        mask_bf = const.tile([P, P], BF16)
+        nc.vector.tensor_copy(out=mask_bf[:], in_=mask_f32[:])
+
+        kT = keep.tile([P, NKV, S], BF16)
+        qT = keep.tile([P, UNITS, REP, P], BF16)
+        v_codes = keep.tile([P, NKV * HD], U32, align_bytes=64)
+        v_scales = keep.tile([P, NKV * HD], U8, align_bytes=64)
+        w_codes = keep.tile([P, PASSES, D], U32, align_bytes=64)
+        w_scales = keep.tile([P, PASSES, D], U8, align_bytes=64)
+        o_codes = keep.tile([P, UNITS, P], U32, align_bytes=64)
+        o_scales = keep.tile([P, UNITS, P], U8, align_bytes=64)
+
+        live = {}
+
+        def is_unit(n):
+            return 0 <= n < UNITS
+
+        def heads_per_bank(n):
+            return BANK // ((n // NKV + 1) * P)
+
+        def opens_bank(k):
+            return 0 <= k < BEATS and (k % REP) % heads_per_bank(k // REP) == 0
+
+        def transpose_k(g):
+            kt_ps = psum.tile([P, QT, P], BF16, tag="x")
+            for t in range(QT):
+                nc.tensor.transpose(kt_ps[:, t, :], k_sb[:, g, t, :], ident_bf[:])
+            nc.vector.tensor_copy(out=kT[:, g, :], in_=kt_ps[:].rearrange("p t k -> p (t k)"))
+
+        def transpose_q(n):
+            if not is_unit(n):
+                return
+            i, g = divmod(n, NKV)
+            qt_ps = psum.tile([P, REP, P], BF16, tag="x")
+            for a in range(REP):
+                nc.tensor.transpose(qt_ps[:, a, :], q_sb[:, i, g * REP + a, :], ident_bf[:])
+            live["qT", n] = qt_ps
+
+        def copy_qT(n):
+            if is_unit(n):
+                nc.scalar.copy(out=qT[:, n], in_=live["qT", n][:])
+
+        def quantise_v():
+            v_grouped = keep.tile([P, NKV * HD * 4], BF16, align_bytes=64)
+            nc.vector.tensor_copy(
+                out=v_grouped[:].rearrange("p (g d t) -> p g d t", g=NKV, t=4),
+                in_=v_sb[:].rearrange("p g t d -> p g d t"),
+            )
+            nc.vector.quantize_mx(out=v_codes[:].bitcast(FP8X4), scales=v_scales[:], in_=v_grouped[:])
+
+        def scores(k):
+            if not opens_bank(k):
+                return
+            n, a0 = divmod(k, REP)
+            i, g = divmod(n, NKV)
+            width = (i + 1) * P
+            s_ps = psum.tile([P, BANK], F32, tag="s")
+            live["s", k] = s_ps
+            for c in range(heads_per_bank(n)):
+                lo = c * width
+                diag = lo + i * P
+                if i > 0:
+                    nc.tensor.matmul(
+                        out=s_ps[:, lo:diag], lhsT=qT[:, n, a0 + c, :], rhs=kT[:, g, 0 : i * P], start=True, stop=True
+                    )
+                nc.tensor.matmul(
+                    out=s_ps[:, diag : diag + P], lhsT=ident_bf[:], rhs=mask_bf[:], start=True, stop=False
+                )
+                nc.tensor.matmul(
+                    out=s_ps[:, diag : diag + P],
+                    lhsT=qT[:, n, a0 + c, :],
+                    rhs=kT[:, g, i * P : (i + 1) * P],
+                    start=False,
+                    stop=True,
+                )
+
+        def row_max(k):
+            if not opens_bank(k):
+                return
+            n, a0 = divmod(k, REP)
+            width = (n // NKV + 1) * P
+            count = heads_per_bank(n)
+            if a0 == 0:
+                live["max", n] = stat.tile([P, REP], F32, name="row_max")
+                live["neg", n] = stat.tile([P, REP], F32, name="neg_max")
+                live["sum", n] = stat.tile([P, REP], F32, name="row_sum")
+            nc.vector.tensor_reduce(
+                out=live["max", n][:, a0 : a0 + count],
+                in_=live["s", k][:, 0 : count * width].rearrange("p (c w) -> p c w", c=count),
+                axis=AXIS.X,
+                op=ALU.max,
+            )
+            nc.gpsimd.tensor_scalar(
+                out=live["neg", n][:, a0 : a0 + count],
+                in0=live["max", n][:, a0 : a0 + count],
+                scalar1=-SCALE,
+                scalar2=0.0,
+                op0=ALU.mult,
+                op1=ALU.add,
+            )
+
+        def exp_head(k):
+            if not 0 <= k < BEATS:
+                return
+            n, a = divmod(k, REP)
+            width = (n // NKV + 1) * P
+            c = a % heads_per_bank(n)
+            nc.scalar.activation(
+                out=e_tiles[(n % 2) * REP + a][:, 0:width],
+                in_=live["s", k - c][:, c * width : (c + 1) * width],
+                func=ACT.Exp,
+                bias=live["neg", n][:, a : a + 1],
+                scale=SCALE,
+                accum_out=live["sum", n][:, a : a + 1],
+            )
+
+        def reciprocal(n):
+            if is_unit(n):
+                live["inv", n] = stat.tile([P, REP], F32, name="inv_sum")
+                nc.vector.reciprocal(out=live["inv", n][:], in_=live["sum", n][:])
+
+        def transpose_e(n):
+            if not is_unit(n):
+                return
+            for half in range(2):
+                et_ps = psum.tile([P, 2, 2, P], F32, tag="x")
+                live["eT", n, half] = et_ps
+                for c in range(2):
+                    e_words = e_tiles[(n % 2) * REP + 2 * half + c][:].bitcast(F32)
+                    for u in range(2):
+                        nc.tensor.transpose(et_ps[:, c, u, :], e_words[:, u * P : (u + 1) * P], ident_f32[:])
+
+        def copy_eT(n):
+            if not is_unit(n):
+                return
+            e_grouped = work.tile([P, REP * P * 4], BF16, align_bytes=64)
+            live["e_grouped", n] = e_grouped
+            words = e_grouped[:].bitcast(F32).rearrange("p (a q u) -> p a q u", a=REP, u=2)
+            nc.vector.tensor_copy(out=words[:, 0:2], in_=live["eT", n, 0][:].rearrange("p c u q -> p c q u"))
+            nc.scalar.copy(out=words[:, 2:4], in_=live["eT", n, 1][:].rearrange("p c u q -> p c q u"))
+
+        def quantise_e(n):
+            if not is_unit(n):
+                return
+            e_codes = work.tile([P, REP * P], U32, align_bytes=64)
+            e_scales = work.tile([P, REP * P], U8, align_bytes=64)
+            live["e_codes", n] = e_codes
+            live["e_scales", n] = e_scales
+            nc.vector.quantize_mx(
+                out=e_codes[:].bitcast(FP8X4), scales=e_scales[:], in_=live["e_grouped", n][:]
+            )
+
+        def e_times_v(n):
+            if not is_unit(n):
+                return
+            g = n % NKV
+            o_ps = psum.tile([P, REP, HD], F32, tag="x")
+            live["o", n] = o_ps
+            for a in range(REP):
+                nc.tensor.matmul_mx(
+                    out=o_ps[:, a, :],
+                    lhsT=live["e_codes", n][:, a * P : (a + 1) * P].bitcast(FP8X4),
+                    lhsT_scale=live["e_scales", n][:, a * P : (a + 1) * P],
+                    rhs=v_codes[:, g * HD : (g + 1) * HD].bitcast(FP8X4),
+                    rhs_scale=v_scales[:, g * HD : (g + 1) * HD],
+                    start=True,
+                    stop=True,
+                )
+
+        def scale_o(n):
+            if not is_unit(n):
+                return
+            o_sb = work.tile([P, REP * HD], BF16)
+            live["o_sb", n] = o_sb
+            nc.vector.tensor_tensor(
+                out=o_sb[:].rearrange("p (a d) -> p a d", a=REP),
+                in0=live["o", n][:],
+                in1=live["inv", n][:].unsqueeze(2).to_broadcast([P, REP, HD]),
+                op=ALU.mult,
+            )
+
+        def transpose_o(n):
+            if not is_unit(n):
+                return
+            o_words = live["o_sb", n][:].bitcast(F32)
+            ot_ps = psum.tile([P, 2, P], F32, tag="x")
+            live["oT", n] = ot_ps
+            for u in range(2):
+                nc.tensor.transpose(ot_ps[:, u, :], o_words[:, u * P : (u + 1) * P], ident_f32[:])
+
+        def copy_oT(n):
+            if not is_unit(n):
+                return
+            o_grouped = work.tile([P, P * 4], BF16, align_bytes=64)
+            live["o_grouped", n] = o_grouped
+            nc.scalar.copy(
+                out=o_grouped[:].bitcast(F32).rearrange("p (q u) -> p q u", u=2),
+                in_=live["oT", n][:].rearrange("p u q -> p q u"),
+            )
+
+        def quantise_o(n):
+            if is_unit(n):
+                nc.vector.quantize_mx(
+                    out=o_codes[:, n, :].bitcast(FP8X4), scales=o_scales[:, n, :], in_=live["o_grouped", n][:]
+                )
+
+        def transpose_wo(f):
+            if not 0 <= f < WO_BANKS:
+                return
+            nt, g = divmod(f // 2, PASSES)
+            wt_ps = psum.tile([P, 2, 2, P], F32, tag="x")
+            live["wT", f] = wt_ps
+            for c in range(2):
+                w_words = wo_sb[:, nt * 4 + (f % 2) * 2 + c, :].bitcast(F32)
+                for u in range(2):
+                    first = g * (K_PASS // 2) + u * P
+                    nc.tensor.transpose(wt_ps[:, c, u, :], w_words[:, first : first + P], ident_f32[:])
+
+        def copy_woT(f):
+            if not 0 <= f < WO_BANKS:
+                return
+            if f % 2 == 0:
+                live["w_grouped", f // 2] = work.tile([P, N_TILE * 4], BF16, align_bytes=64, name="w_grouped", bufs=4)
+            words = live["w_grouped", f // 2][:].bitcast(F32).rearrange("p (b n u) -> p b n u", b=4, u=2)
+            half = words[:, (f % 2) * 2 : (f % 2) * 2 + 2]
+            source = live["wT", f][:].rearrange("p c u n -> p c n u")
+            if f % 4 == 3:
+                nc.vector.tensor_copy(out=half, in_=source)
+            else:
+                nc.scalar.copy(out=half, in_=source)
+
+        def quantise_wo(f):
+            if not 0 <= f < WO_BANKS or f % 2 == 0:
+                return
+            nt, g = divmod(f // 2, PASSES)
+            cols = slice(nt * N_TILE, (nt + 1) * N_TILE)
+            nc.vector.quantize_mx(
+                out=w_codes[:, g, cols].bitcast(FP8X4), scales=w_scales[:, g, cols], in_=live["w_grouped", f // 2][:]
+            )
+
+        def project_pass(acc, i, nt, g):
+            cols = slice(nt * N_TILE, (nt + 1) * N_TILE)
+            nc.tensor.matmul_mx(
+                out=acc[:],
+                lhsT=o_codes[:, i * NKV + g, :].bitcast(FP8X4),
+                lhsT_scale=o_scales[:, i * NKV + g, :],
+                rhs=w_codes[:, g, cols].bitcast(FP8X4),
+                rhs_scale=w_scales[:, g, cols],
+                start=(g == 0),
+                stop=(g == PASSES - 1),
+            )
+
+        def store(acc, i, nt, engine_copy):
+            out_sb = work.tile([P, N_TILE], F32, bufs=4)
+            engine_copy(out=out_sb[:], in_=acc[:])
+            nc.sync.dma_start(out=out[0, i * P : (i + 1) * P, nt * N_TILE : (nt + 1) * N_TILE], in_=out_sb[:])
+
+        def project(job):
+            i, nt = divmod(job, NT)
+            f_ps = psum.tile([P, N_TILE], F32, tag="x")
+            live["f", job] = f_ps
+            for g in range(PASSES):
+                project_pass(f_ps, i, nt, g)
+
+        def project_beat(job):
+            if job < 2 * NT:
+                return 33 + 3 * job
+            return 57 + 2 * (job - 2 * NT)
+
+        for g in range(NKV):
+            transpose_k(g)
+            transpose_q(g)
+            copy_qT(g)
+        for k in range(3):
+            scores(k)
+        for k in range(2):
+            row_max(k)
+
+        last = []
+        for beat in range(BEATS + DRAIN):
+            n, a = divmod(beat, REP)
+            exp_head(beat)
+            scores(beat + 3)
+            row_max(beat + 2)
+            if beat == 4:
+                quantise_v()
+            if a == 0:
+                transpose_e(n - 1)
+                scale_o(n - 2)
+            elif a == 1:
+                copy_eT(n - 1)
+                transpose_o(n - 2)
+                if n + 2 >= NKV:
+                    transpose_q(n + 2)
+                reciprocal(n - 1)
+            elif a == 2:
+                quantise_e(n - 1)
+                copy_oT(n - 2)
+                if n + 2 >= NKV:
+                    copy_qT(n + 2)
+            for job in range(3 * NT):
+                if project_beat(job) == beat:
+                    project(job)
+                if project_beat(job) + 1 == beat:
+                    store(live["f", job], job // NT, job % NT, nc.scalar.copy)
+            if a == 3:
+                e_times_v(n - 1)
+                quantise_o(n - 2)
+            if a == 0 and n >= UNITS:
+                if n == UNITS:
+                    for nt in range(NT):
+                        last.append(psum.tile([P, N_TILE], F32, tag="s", name="last%d" % nt))
+                        project_pass(last[nt], QT - 1, nt, 0)
+                for nt in range(NT):
+                    project_pass(last[nt], QT - 1, nt, n - UNITS + 1)
+            transpose_wo(beat - WO_FIRST_BEAT)
+            copy_woT(beat - WO_FIRST_BEAT - 1)
+            quantise_wo(beat - WO_FIRST_BEAT - 2)
+        for nt in range(NT):
+            store(last[nt], QT - 1, nt, nc.vector.tensor_copy if nt % 2 else nc.scalar.copy)

@@ -32,8 +32,8 @@ NEG = -1.0e30
 UNITS = QT * NKV
 BEATS = UNITS * REP
 WO_BANKS = 2 * NT * PASSES
-WO_FIRST_BEAT = 8
-DRAIN = 9
+WO_FIRST_BEAT = 10
+NARROW = 2 * NKV
 
 FLOPS = 2 * NH * S * S * HD * 2 + 2 * S * D * D
 
@@ -51,6 +51,7 @@ def tile_rlaattention_pb_kernel(tc, q_rot, k_rot, v, Wo, out):
         k_sb = keep.tile([P, NKV, QT, HD], BF16)
         q_sb = keep.tile([P, QT, NH, HD], BF16)
         v_sb = keep.tile([P, NKV, 4, HD], BF16)
+        vp_sb = keep.tile([P, NKV, 4, HD], BF16)
         wo_sb = keep.tile([P, D // P, D], BF16)
 
         def load_q(i, h0, h1):
@@ -64,21 +65,30 @@ def tile_rlaattention_pb_kernel(tc, q_rot, k_rot, v, Wo, out):
                 in_=Wo[256 * c : 256 * (c + 1), :].rearrange("(b p) k -> p b k", p=P),
             )
 
-        for g in range(NKV):
+        def load_k_and_first_q(g):
             nc.sync.dma_start(out=k_sb[:, g], in_=k_rot[0, g].rearrange("(t p) d -> p t d", p=P))
             load_q(0, g * REP, (g + 1) * REP)
+
+        load_k_and_first_q(0)
+        load_k_and_first_q(1)
+        for c in range(2):
+            for u in range(2):
+                nc.sync.dma_start(
+                    out=vp_sb[64 * c : 64 * (c + 1), :, 2 * u : 2 * u + 2, :].rearrange("w g e d -> w g (e d)"),
+                    in_=v[0, :, P * u : P * (u + 1), :].rearrange("g (w e) d -> w g (e d)", e=2),
+                )
+        load_k_and_first_q(2)
+        load_k_and_first_q(3)
+        load_q(1, 0, NH)
+        for c in range(4):
+            load_wo(c)
         nc.sync.dma_start(
             out=v_sb[:].rearrange("p g (u e) d -> p (g u) (e d)", u=2),
             in_=v[0].rearrange("g (u p e) d -> p (g u) (e d)", u=2, p=P, e=2),
         )
-        load_wo(0)
-        load_wo(1)
-        load_q(1, 0, NH)
-        for c in range(2, 6):
-            load_wo(c)
         load_q(2, 0, NH)
-        load_wo(6)
-        load_wo(7)
+        for c in range(4, 8):
+            load_wo(c)
         load_q(3, 0, NH)
 
         ident_bf = const.tile([P, P], BF16)
@@ -97,9 +107,18 @@ def tile_rlaattention_pb_kernel(tc, q_rot, k_rot, v, Wo, out):
             channel_multiplier=1,
         )
 
-        e_tiles = [keep.tile([P, S], BF16, name="e%d" % slot) for slot in range(2 * REP)]
-        for e_tile in e_tiles:
-            nc.vector.memset(e_tile[:], 0.0)
+        e_wide = [keep.tile([P, S], BF16, name="e_wide%d" % slot) for slot in range(2 * REP)]
+        e_pair = [keep.tile([P, S], BF16, name="e_pair%d" % slot) for slot in range(REP)]
+        for e_tile in e_wide:
+            nc.vector.memset(e_tile[:, 3 * P : S], 0.0)
+        for e_tile in e_pair:
+            nc.vector.memset(e_tile[:, 2 * P : S], 0.0)
+        vp_grouped = [
+            work.tile([P, N_TILE * 4], BF16, align_bytes=64, name="vp_grouped%d" % half, tag="w_grouped")
+            for half in range(2)
+        ]
+        for half in range(2):
+            nc.vector.memset(vp_grouped[half][:], 0.0)
         mask_bf = const.tile([P, P], BF16)
         nc.vector.tensor_copy(out=mask_bf[:], in_=mask_f32[:])
 
@@ -107,6 +126,8 @@ def tile_rlaattention_pb_kernel(tc, q_rot, k_rot, v, Wo, out):
         qT = keep.tile([P, UNITS, REP, P], BF16)
         v_codes = keep.tile([P, NKV * HD], U32, align_bytes=64)
         v_scales = keep.tile([P, NKV * HD], U8, align_bytes=64)
+        vp_codes = keep.tile([P, NKV * 2 * HD], U32, align_bytes=64)
+        vp_scales = keep.tile([P, NKV * 2 * HD], U8, align_bytes=64)
         w_codes = keep.tile([P, PASSES, D], U32, align_bytes=64)
         w_scales = keep.tile([P, PASSES, D], U8, align_bytes=64)
         o_codes = keep.tile([P, UNITS, P], U32, align_bytes=64)
@@ -124,6 +145,8 @@ def tile_rlaattention_pb_kernel(tc, q_rot, k_rot, v, Wo, out):
             return 0 <= k < BEATS and (k % REP) % heads_per_bank(k // REP) == 0
 
         def transpose_k(g):
+            if g >= NKV:
+                return
             kt_ps = psum.tile([P, QT, P], BF16, tag="x")
             for t in range(QT):
                 nc.tensor.transpose(kt_ps[:, t, :], k_sb[:, g, t, :], ident_bf[:])
@@ -142,8 +165,22 @@ def tile_rlaattention_pb_kernel(tc, q_rot, k_rot, v, Wo, out):
             if is_unit(n):
                 nc.scalar.copy(out=qT[:, n], in_=live["qT", n][:])
 
+        def quantise_v_pair():
+            for half in range(2):
+                blocks = vp_grouped[half][:].rearrange("p (g c d t) -> p g c d t", g=2, c=2, t=4)
+                for c in range(2):
+                    rows = slice(64 * c, 64 * (c + 1))
+                    nc.vector.tensor_copy(
+                        out=blocks[rows, :, c], in_=vp_sb[rows, 2 * half : 2 * half + 2].rearrange("p g t d -> p g d t")
+                    )
+            for half in range(2):
+                cols = slice(half * N_TILE, (half + 1) * N_TILE)
+                nc.vector.quantize_mx(
+                    out=vp_codes[:, cols].bitcast(FP8X4), scales=vp_scales[:, cols], in_=vp_grouped[half][:]
+                )
+
         def quantise_v():
-            v_grouped = keep.tile([P, NKV * HD * 4], BF16, align_bytes=64)
+            v_grouped = work.tile([P, N_TILE * 4], BF16, align_bytes=64, tag="w_grouped")
             nc.vector.tensor_copy(
                 out=v_grouped[:].rearrange("p (g d t) -> p g d t", g=NKV, t=4),
                 in_=v_sb[:].rearrange("p g t d -> p g d t"),
@@ -207,9 +244,14 @@ def tile_rlaattention_pb_kernel(tc, q_rot, k_rot, v, Wo, out):
             n, a = divmod(k, REP)
             width = (n // NKV + 1) * P
             c = a % heads_per_bank(n)
+            if n < NARROW:
+                pair = e_pair[(n % 2) * 2 + a // 2][:].rearrange("p (u c k) -> p u c k", u=2, c=2)
+                e_out = pair[:, 0 : width // P, a % 2, :]
+            else:
+                e_out = e_wide[(n % 2) * REP + a][:, 0:width].rearrange("p (u k) -> p u k", k=P)
             nc.scalar.activation(
-                out=e_tiles[(n % 2) * REP + a][:, 0:width],
-                in_=live["s", k - c][:, c * width : (c + 1) * width],
+                out=e_out,
+                in_=live["s", k - c][:, c * width : (c + 1) * width].rearrange("p (u k) -> p u k", k=P),
                 func=ACT.Exp,
                 bias=live["neg", n][:, a : a + 1],
                 scale=SCALE,
@@ -224,11 +266,12 @@ def tile_rlaattention_pb_kernel(tc, q_rot, k_rot, v, Wo, out):
         def transpose_e(n):
             if not is_unit(n):
                 return
-            for half in range(2):
+            tiles = e_pair[(n % 2) * 2 : (n % 2) * 2 + 2] if n < NARROW else e_wide[(n % 2) * REP : (n % 2 + 1) * REP]
+            for half in range(len(tiles) // 2):
                 et_ps = psum.tile([P, 2, 2, P], F32, tag="x")
                 live["eT", n, half] = et_ps
                 for c in range(2):
-                    e_words = e_tiles[(n % 2) * REP + 2 * half + c][:].bitcast(F32)
+                    e_words = tiles[2 * half + c][:].bitcast(F32)
                     for u in range(2):
                         nc.tensor.transpose(et_ps[:, c, u, :], e_words[:, u * P : (u + 1) * P], ident_f32[:])
 
@@ -238,8 +281,9 @@ def tile_rlaattention_pb_kernel(tc, q_rot, k_rot, v, Wo, out):
             e_grouped = work.tile([P, REP * P * 4], BF16, align_bytes=64)
             live["e_grouped", n] = e_grouped
             words = e_grouped[:].bitcast(F32).rearrange("p (a q u) -> p a q u", a=REP, u=2)
-            nc.vector.tensor_copy(out=words[:, 0:2], in_=live["eT", n, 0][:].rearrange("p c u q -> p c q u"))
-            nc.scalar.copy(out=words[:, 2:4], in_=live["eT", n, 1][:].rearrange("p c u q -> p c q u"))
+            nc.scalar.copy(out=words[:, 0:2], in_=live["eT", n, 0][:].rearrange("p c u q -> p c q u"))
+            if n >= NARROW:
+                nc.vector.tensor_copy(out=words[:, 2:4], in_=live["eT", n, 1][:].rearrange("p c u q -> p c q u"))
 
         def quantise_e(n):
             if not is_unit(n):
@@ -248,23 +292,27 @@ def tile_rlaattention_pb_kernel(tc, q_rot, k_rot, v, Wo, out):
             e_scales = work.tile([P, REP * P], U8, align_bytes=64)
             live["e_codes", n] = e_codes
             live["e_scales", n] = e_scales
+            count = (2 if n < NARROW else REP) * P
             nc.vector.quantize_mx(
-                out=e_codes[:].bitcast(FP8X4), scales=e_scales[:], in_=live["e_grouped", n][:]
+                out=e_codes[:, 0:count].bitcast(FP8X4),
+                scales=e_scales[:, 0:count],
+                in_=live["e_grouped", n][:, 0 : 4 * count],
             )
 
         def e_times_v(n):
             if not is_unit(n):
                 return
             g = n % NKV
-            o_ps = psum.tile([P, REP, HD], F32, tag="x")
+            o_ps = psum.tile([P, REP * HD], F32, tag="x")
             live["o", n] = o_ps
-            for a in range(REP):
+            codes, scales, width = (vp_codes, vp_scales, 2 * HD) if n < NARROW else (v_codes, v_scales, HD)
+            for m in range(REP * HD // width):
                 nc.tensor.matmul_mx(
-                    out=o_ps[:, a, :],
-                    lhsT=live["e_codes", n][:, a * P : (a + 1) * P].bitcast(FP8X4),
-                    lhsT_scale=live["e_scales", n][:, a * P : (a + 1) * P],
-                    rhs=v_codes[:, g * HD : (g + 1) * HD].bitcast(FP8X4),
-                    rhs_scale=v_scales[:, g * HD : (g + 1) * HD],
+                    out=o_ps[:, m * width : (m + 1) * width],
+                    lhsT=live["e_codes", n][:, m * P : (m + 1) * P].bitcast(FP8X4),
+                    lhsT_scale=live["e_scales", n][:, m * P : (m + 1) * P],
+                    rhs=codes[:, g * width : (g + 1) * width].bitcast(FP8X4),
+                    rhs_scale=scales[:, g * width : (g + 1) * width],
                     start=True,
                     stop=True,
                 )
@@ -276,7 +324,7 @@ def tile_rlaattention_pb_kernel(tc, q_rot, k_rot, v, Wo, out):
             live["o_sb", n] = o_sb
             nc.vector.tensor_tensor(
                 out=o_sb[:].rearrange("p (a d) -> p a d", a=REP),
-                in0=live["o", n][:],
+                in0=live["o", n][:].rearrange("p (a d) -> p a d", a=REP),
                 in1=live["inv", n][:].unsqueeze(2).to_broadcast([P, REP, HD]),
                 op=ALU.mult,
             )
@@ -322,7 +370,7 @@ def tile_rlaattention_pb_kernel(tc, q_rot, k_rot, v, Wo, out):
             if not 0 <= f < WO_BANKS:
                 return
             if f % 2 == 0:
-                live["w_grouped", f // 2] = work.tile([P, N_TILE * 4], BF16, align_bytes=64, name="w_grouped", bufs=4)
+                live["w_grouped", f // 2] = work.tile([P, N_TILE * 4], BF16, align_bytes=64, name="w_grouped")
             words = live["w_grouped", f // 2][:].bitcast(F32).rearrange("p (b n u) -> p b n u", b=4, u=2)
             half = words[:, (f % 2) * 2 : (f % 2) * 2 + 2]
             source = live["wT", f][:].rearrange("p c u n -> p c n u")
@@ -365,26 +413,32 @@ def tile_rlaattention_pb_kernel(tc, q_rot, k_rot, v, Wo, out):
                 project_pass(f_ps, i, nt, g)
 
         def project_beat(job):
-            if job < 2 * NT:
-                return 33 + 3 * job
-            return 57 + 2 * (job - 2 * NT)
+            i, nt = divmod(job, NT)
+            wo_ready = WO_FIRST_BEAT + (WO_BANKS // NT) * (nt + 1) + 4
+            o_ready = BEATS // QT * (i + 1) + 2 * REP
+            return max(wo_ready, o_ready + 2 * nt)
 
-        for g in range(NKV):
-            transpose_k(g)
-            transpose_q(g)
-            copy_qT(g)
-        for k in range(3):
-            scores(k)
-        for k in range(2):
-            row_max(k)
+        def project_last(g):
+            for nt in range(NT):
+                project_pass(last[nt], QT - 1, nt, g)
 
-        last = []
-        for beat in range(BEATS + DRAIN):
+        transpose_k(0)
+        transpose_q(0)
+        copy_qT(0)
+        scores(0)
+        row_max(0)
+        transpose_k(1)
+        transpose_q(1)
+        copy_qT(1)
+
+        for beat in range(BEATS):
             n, a = divmod(beat, REP)
             exp_head(beat)
             scores(beat + 3)
             row_max(beat + 2)
-            if beat == 4:
+            if beat == 3:
+                quantise_v_pair()
+            if beat == 6 * REP:
                 quantise_v()
             if a == 0:
                 transpose_e(n - 1)
@@ -392,14 +446,13 @@ def tile_rlaattention_pb_kernel(tc, q_rot, k_rot, v, Wo, out):
             elif a == 1:
                 copy_eT(n - 1)
                 transpose_o(n - 2)
-                if n + 2 >= NKV:
-                    transpose_q(n + 2)
+                transpose_k(n + 2)
+                transpose_q(n + 2)
                 reciprocal(n - 1)
             elif a == 2:
                 quantise_e(n - 1)
                 copy_oT(n - 2)
-                if n + 2 >= NKV:
-                    copy_qT(n + 2)
+                copy_qT(n + 2)
             for job in range(3 * NT):
                 if project_beat(job) == beat:
                     project(job)
@@ -408,15 +461,27 @@ def tile_rlaattention_pb_kernel(tc, q_rot, k_rot, v, Wo, out):
             if a == 3:
                 e_times_v(n - 1)
                 quantise_o(n - 2)
-            if a == 0 and n >= UNITS:
-                if n == UNITS:
-                    for nt in range(NT):
-                        last.append(psum.tile([P, N_TILE], F32, tag="s", name="last%d" % nt))
-                        project_pass(last[nt], QT - 1, nt, 0)
-                for nt in range(NT):
-                    project_pass(last[nt], QT - 1, nt, n - UNITS + 1)
             transpose_wo(beat - WO_FIRST_BEAT)
             copy_woT(beat - WO_FIRST_BEAT - 1)
             quantise_wo(beat - WO_FIRST_BEAT - 2)
+
+        last = [psum.tile([P, N_TILE], F32, tag="s", name="last%d" % nt) for nt in range(NT)]
+        transpose_e(UNITS - 1)
+        scale_o(UNITS - 2)
+        copy_eT(UNITS - 1)
+        transpose_o(UNITS - 2)
+        reciprocal(UNITS - 1)
+        project_last(0)
+        quantise_e(UNITS - 1)
+        copy_oT(UNITS - 2)
+        project_last(1)
+        e_times_v(UNITS - 1)
+        quantise_o(UNITS - 2)
+        scale_o(UNITS - 1)
+        project_last(2)
+        transpose_o(UNITS - 1)
+        copy_oT(UNITS - 1)
+        quantise_o(UNITS - 1)
+        project_last(3)
         for nt in range(NT):
             store(last[nt], QT - 1, nt, nc.vector.tensor_copy if nt % 2 else nc.scalar.copy)

@@ -8,6 +8,7 @@ BF16 = mybir.dt.bfloat16
 F32 = mybir.dt.float32
 U32 = mybir.dt.uint32
 U8 = mybir.dt.uint8
+I32 = mybir.dt.int32
 FP8X4 = mybir.dt.float8_e4m3fn_x4
 ACT = mybir.ActivationFunctionType
 ALU = mybir.AluOpType
@@ -31,8 +32,16 @@ NEG = -1.0e30
 
 UNITS = QT * NKV
 BEATS = UNITS * REP
-WO_BANKS = 2 * NT * PASSES
-WO_FIRST_BEAT = 10
+WO_ROWS = 256
+WO_BANKS = D // WO_ROWS * PASSES
+WO_FIRST_BEAT = 2
+
+TRANSPOSE_Q, COPY_Q = -6, -5
+SCORES_AHEAD, MAX_AHEAD = 3, 2
+TRANSPOSE_E, COPY_E, QUANTISE_E, TIMES_V = 4, 5, 6, 7
+SCALE_O, TRANSPOSE_O, COPY_O, QUANTISE_O = 8, 9, 10, 11
+COPY_WO, QUANTISE_WO = 1, 3
+QUANTISE_VP, QUANTISE_V = 1, 24
 NARROW = 2 * NKV
 
 FLOPS = 2 * NH * S * S * HD * 2 + 2 * S * D * D
@@ -78,17 +87,19 @@ def tile_rlaattention_pb_kernel(tc, q_rot, k_rot, v, Wo, out):
                     in_=v[0, :, P * u : P * (u + 1), :].rearrange("g (w e) d -> w g (e d)", e=2),
                 )
         load_k_and_first_q(2)
+        load_wo(0)
         load_k_and_first_q(3)
+        load_wo(1)
         load_q(1, 0, NH)
-        for c in range(4):
+        for c in range(2, 5):
+            load_wo(c)
+        load_q(2, 0, NH)
+        for c in range(5, 8):
             load_wo(c)
         nc.sync.dma_start(
             out=v_sb[:].rearrange("p g (u e) d -> p (g u) (e d)", u=2),
             in_=v[0].rearrange("g (u p e) d -> p (g u) (e d)", u=2, p=P, e=2),
         )
-        load_q(2, 0, NH)
-        for c in range(4, 8):
-            load_wo(c)
         load_q(3, 0, NH)
 
         ident_bf = const.tile([P, P], BF16)
@@ -113,12 +124,6 @@ def tile_rlaattention_pb_kernel(tc, q_rot, k_rot, v, Wo, out):
             nc.vector.memset(e_tile[:, 3 * P : S], 0.0)
         for e_tile in e_pair:
             nc.vector.memset(e_tile[:, 2 * P : S], 0.0)
-        vp_grouped = [
-            work.tile([P, N_TILE * 4], BF16, align_bytes=64, name="vp_grouped%d" % half, tag="w_grouped")
-            for half in range(2)
-        ]
-        for half in range(2):
-            nc.vector.memset(vp_grouped[half][:], 0.0)
         mask_bf = const.tile([P, P], BF16)
         nc.vector.tensor_copy(out=mask_bf[:], in_=mask_f32[:])
 
@@ -126,7 +131,10 @@ def tile_rlaattention_pb_kernel(tc, q_rot, k_rot, v, Wo, out):
         qT = keep.tile([P, UNITS, REP, P], BF16)
         v_codes = keep.tile([P, NKV * HD], U32, align_bytes=64)
         v_scales = keep.tile([P, NKV * HD], U8, align_bytes=64)
+        vd_codes = keep.tile([P, NKV * HD], U32, align_bytes=64)
+        vd_scales = keep.tile([P, NKV * HD], U8, align_bytes=64)
         vp_codes = keep.tile([P, NKV * 2 * HD], U32, align_bytes=64)
+        nc.vector.memset(vp_codes[:].bitcast(I32), 0)
         vp_scales = keep.tile([P, NKV * 2 * HD], U8, align_bytes=64)
         w_codes = keep.tile([P, PASSES, D], U32, align_bytes=64)
         w_scales = keep.tile([P, PASSES, D], U8, align_bytes=64)
@@ -165,27 +173,28 @@ def tile_rlaattention_pb_kernel(tc, q_rot, k_rot, v, Wo, out):
             if is_unit(n):
                 nc.scalar.copy(out=qT[:, n], in_=live["qT", n][:])
 
-        def quantise_v_pair():
-            for half in range(2):
-                blocks = vp_grouped[half][:].rearrange("p (g c d t) -> p g c d t", g=2, c=2, t=4)
-                for c in range(2):
-                    rows = slice(64 * c, 64 * (c + 1))
-                    nc.vector.tensor_copy(
-                        out=blocks[rows, :, c], in_=vp_sb[rows, 2 * half : 2 * half + 2].rearrange("p g t d -> p g d t")
-                    )
-            for half in range(2):
-                cols = slice(half * N_TILE, (half + 1) * N_TILE)
-                nc.vector.quantize_mx(
-                    out=vp_codes[:, cols].bitcast(FP8X4), scales=vp_scales[:, cols], in_=vp_grouped[half][:]
-                )
-
-        def quantise_v():
-            v_grouped = work.tile([P, N_TILE * 4], BF16, align_bytes=64, tag="w_grouped")
+        def group_v(source):
+            v_grouped = work.tile([P, N_TILE * 4], BF16, align_bytes=64, bufs=1)
             nc.vector.tensor_copy(
                 out=v_grouped[:].rearrange("p (g d t) -> p g d t", g=NKV, t=4),
-                in_=v_sb[:].rearrange("p g t d -> p g d t"),
+                in_=source[:].rearrange("p g t d -> p g d t"),
             )
-            nc.vector.quantize_mx(out=v_codes[:].bitcast(FP8X4), scales=v_scales[:], in_=v_grouped[:])
+            return v_grouped
+
+        def quantise_v(v_grouped, codes, scales):
+            nc.vector.quantize_mx(out=codes[:].bitcast(FP8X4), scales=scales[:], in_=v_grouped[:])
+
+        def spread_v_pair():
+            for c in range(2):
+                rows = slice(64 * c, 64 * (c + 1))
+                nc.vector.tensor_copy(
+                    out=vp_codes[rows].bitcast(I32).rearrange("p (g c d) -> p g c d", g=NKV, c=2)[:, :, c],
+                    in_=vd_codes[rows].bitcast(I32).rearrange("p (g d) -> p g d", g=NKV),
+                )
+                nc.vector.tensor_copy(
+                    out=vp_scales[:].rearrange("p (g c d) -> p g c d", g=NKV, c=2)[:, :, c],
+                    in_=vd_scales[:].rearrange("p (g d) -> p g d", g=NKV),
+                )
 
         def scores(k):
             if not opens_bank(k):
@@ -357,35 +366,34 @@ def tile_rlaattention_pb_kernel(tc, q_rot, k_rot, v, Wo, out):
         def transpose_wo(f):
             if not 0 <= f < WO_BANKS:
                 return
-            nt, g = divmod(f // 2, PASSES)
+            c, g = divmod(f, PASSES)
             wt_ps = psum.tile([P, 2, 2, P], F32, tag="x")
             live["wT", f] = wt_ps
-            for c in range(2):
-                w_words = wo_sb[:, nt * 4 + (f % 2) * 2 + c, :].bitcast(F32)
+            for b in range(2):
+                w_words = wo_sb[:, 2 * c + b, :].bitcast(F32)
                 for u in range(2):
                     first = g * (K_PASS // 2) + u * P
-                    nc.tensor.transpose(wt_ps[:, c, u, :], w_words[:, first : first + P], ident_f32[:])
+                    nc.tensor.transpose(wt_ps[:, b, u, :], w_words[:, first : first + P], ident_f32[:])
 
         def copy_woT(f):
             if not 0 <= f < WO_BANKS:
                 return
-            if f % 2 == 0:
-                live["w_grouped", f // 2] = work.tile([P, N_TILE * 4], BF16, align_bytes=64, name="w_grouped")
-            words = live["w_grouped", f // 2][:].bitcast(F32).rearrange("p (b n u) -> p b n u", b=4, u=2)
-            half = words[:, (f % 2) * 2 : (f % 2) * 2 + 2]
-            source = live["wT", f][:].rearrange("p c u n -> p c n u")
-            if f % 4 == 3:
-                nc.vector.tensor_copy(out=half, in_=source)
+            w_grouped = work.tile([P, WO_ROWS * 4], BF16, align_bytes=64, bufs=4)
+            live["w_grouped", f] = w_grouped
+            words = w_grouped[:].bitcast(F32).rearrange("p (b n u) -> p b n u", b=2, u=2)
+            source = live["wT", f][:].rearrange("p b u n -> p b n u")
+            if f % 4 == 0:
+                nc.vector.tensor_copy(out=words, in_=source)
             else:
-                nc.scalar.copy(out=half, in_=source)
+                nc.scalar.copy(out=words, in_=source)
 
         def quantise_wo(f):
-            if not 0 <= f < WO_BANKS or f % 2 == 0:
+            if not 0 <= f < WO_BANKS:
                 return
-            nt, g = divmod(f // 2, PASSES)
-            cols = slice(nt * N_TILE, (nt + 1) * N_TILE)
+            c, g = divmod(f, PASSES)
+            cols = slice(c * WO_ROWS, (c + 1) * WO_ROWS)
             nc.vector.quantize_mx(
-                out=w_codes[:, g, cols].bitcast(FP8X4), scales=w_scales[:, g, cols], in_=live["w_grouped", f // 2][:]
+                out=w_codes[:, g, cols].bitcast(FP8X4), scales=w_scales[:, g, cols], in_=live["w_grouped", f][:]
             )
 
         def project_pass(acc, i, nt, g):
@@ -401,7 +409,7 @@ def tile_rlaattention_pb_kernel(tc, q_rot, k_rot, v, Wo, out):
             )
 
         def store(acc, i, nt, engine_copy):
-            out_sb = work.tile([P, N_TILE], F32, bufs=4)
+            out_sb = work.tile([P, N_TILE], F32, bufs=5)
             engine_copy(out=out_sb[:], in_=acc[:])
             nc.sync.dma_start(out=out[0, i * P : (i + 1) * P, nt * N_TILE : (nt + 1) * N_TILE], in_=out_sb[:])
 
@@ -412,76 +420,75 @@ def tile_rlaattention_pb_kernel(tc, q_rot, k_rot, v, Wo, out):
             for g in range(PASSES):
                 project_pass(f_ps, i, nt, g)
 
-        def project_beat(job):
-            i, nt = divmod(job, NT)
-            wo_ready = WO_FIRST_BEAT + (WO_BANKS // NT) * (nt + 1) + 4
-            o_ready = BEATS // QT * (i + 1) + 2 * REP
-            return max(wo_ready, o_ready + 2 * nt)
+        def project_beats():
+            beats = {}
+            free = 0
+            for job in range(3 * NT):
+                i, nt = divmod(job, NT)
+                wo_ready = WO_FIRST_BEAT + (WO_BANKS // NT) * (nt + 1) + QUANTISE_WO
+                o_ready = REP * (NKV * i + NKV - 1) + QUANTISE_O + 1
+                beat = max(wo_ready, o_ready, free)
+                while beat % REP != 1:
+                    beat += 1
+                beats[beat] = job
+                free = beat + REP
+            return beats
 
         def project_last(g):
             for nt in range(NT):
                 project_pass(last[nt], QT - 1, nt, g)
 
+        jobs = project_beats()
+        last_passes = {66: 0, 68: 1, 71: 2}
+        last = []
+
+        def due(beat, delay):
+            n, rest = divmod(beat - delay, REP)
+            return n if rest == 0 and is_unit(n) else -1
+
         transpose_k(0)
         transpose_q(0)
         copy_qT(0)
-        scores(0)
-        row_max(0)
-        transpose_k(1)
-        transpose_q(1)
-        copy_qT(1)
-
-        for beat in range(BEATS):
-            n, a = divmod(beat, REP)
+        for beat in range(-SCORES_AHEAD, BEATS + QUANTISE_O):
+            quantise_o(due(beat, QUANTISE_O))
+            copy_oT(due(beat, COPY_O))
+            transpose_o(due(beat, TRANSPOSE_O))
+            scale_o(due(beat, SCALE_O))
+            e_times_v(due(beat, TIMES_V))
+            quantise_e(due(beat, QUANTISE_E))
+            copy_eT(due(beat, COPY_E))
+            transpose_e(due(beat, TRANSPOSE_E))
             exp_head(beat)
-            scores(beat + 3)
-            row_max(beat + 2)
-            if beat == 3:
-                quantise_v_pair()
-            if beat == 6 * REP:
-                quantise_v()
-            if a == 0:
-                transpose_e(n - 1)
-                scale_o(n - 2)
-            elif a == 1:
-                copy_eT(n - 1)
-                transpose_o(n - 2)
-                transpose_k(n + 2)
-                transpose_q(n + 2)
-                reciprocal(n - 1)
-            elif a == 2:
-                quantise_e(n - 1)
-                copy_oT(n - 2)
-                copy_qT(n + 2)
-            for job in range(3 * NT):
-                if project_beat(job) == beat:
-                    project(job)
-                if project_beat(job) + 1 == beat:
-                    store(live["f", job], job // NT, job % NT, nc.scalar.copy)
-            if a == 3:
-                e_times_v(n - 1)
-                quantise_o(n - 2)
+            scores(beat + SCORES_AHEAD)
+            row_max(beat + MAX_AHEAD)
+            reciprocal(due(beat, COPY_E))
+            if beat in jobs:
+                project(jobs[beat])
+            if beat in last_passes:
+                if not last:
+                    last.extend(psum.tile([P, N_TILE], F32, tag="s", name="last%d" % nt) for nt in range(NT))
+                project_last(last_passes[beat])
+            for n in range(1, UNITS):
+                if max(REP * n + COPY_Q, -SCORES_AHEAD) == beat:
+                    copy_qT(n)
+                if max(REP * n + TRANSPOSE_Q, -SCORES_AHEAD) == beat:
+                    transpose_k(n)
+                    transpose_q(n)
+            if beat - 1 in jobs:
+                job = jobs[beat - 1]
+                store(live["f", job], job // NT, job % NT, nc.scalar.copy)
+            copy_woT(beat - WO_FIRST_BEAT - COPY_WO)
+            quantise_wo(beat - WO_FIRST_BEAT - QUANTISE_WO)
             transpose_wo(beat - WO_FIRST_BEAT)
-            copy_woT(beat - WO_FIRST_BEAT - 1)
-            quantise_wo(beat - WO_FIRST_BEAT - 2)
-
-        last = [psum.tile([P, N_TILE], F32, tag="s", name="last%d" % nt) for nt in range(NT)]
-        transpose_e(UNITS - 1)
-        scale_o(UNITS - 2)
-        copy_eT(UNITS - 1)
-        transpose_o(UNITS - 2)
-        reciprocal(UNITS - 1)
-        project_last(0)
-        quantise_e(UNITS - 1)
-        copy_oT(UNITS - 2)
-        project_last(1)
-        e_times_v(UNITS - 1)
-        quantise_o(UNITS - 2)
-        scale_o(UNITS - 1)
-        project_last(2)
-        transpose_o(UNITS - 1)
-        copy_oT(UNITS - 1)
+            if beat == QUANTISE_VP:
+                vp_grouped = group_v(vp_sb)
+            if beat == QUANTISE_VP + 1:
+                quantise_v(vp_grouped, vd_codes, vd_scales)
+            if beat == QUANTISE_VP + 2:
+                spread_v_pair()
+            if beat == QUANTISE_V:
+                quantise_v(group_v(v_sb), v_codes, v_scales)
         quantise_o(UNITS - 1)
-        project_last(3)
+        project_last(PASSES - 1)
         for nt in range(NT):
             store(last[nt], QT - 1, nt, nc.vector.tensor_copy if nt % 2 else nc.scalar.copy)

@@ -34,14 +34,16 @@ UNITS = QT * NKV
 BEATS = UNITS * REP
 WO_ROWS = 256
 WO_BANKS = D // WO_ROWS * PASSES
-WO_FIRST_BEAT = 2
+WO_FIRST_BEAT = 8
+WO_PER_BEAT = (1, 1, 2, 1)
 
-TRANSPOSE_Q, COPY_Q = -6, -5
+TRANSPOSE_Q = -6
 SCORES_AHEAD, MAX_AHEAD = 3, 2
 TRANSPOSE_E, COPY_E, QUANTISE_E, TIMES_V = 4, 5, 6, 7
 SCALE_O, TRANSPOSE_O, COPY_O, QUANTISE_O = 8, 9, 10, 11
 COPY_WO, QUANTISE_WO = 1, 3
-QUANTISE_VP, QUANTISE_V = 1, 24
+PREPARE_VP, PREPARE_V = 1, 28
+SECOND_Q, SECOND_Q_STEP = 25, 3
 NARROW = 2 * NKV
 
 FLOPS = 2 * NH * S * S * HD * 2 + 2 * S * D * D
@@ -58,14 +60,19 @@ def tile_rlaattention_pb_kernel(tc, q_rot, k_rot, v, Wo, out):
         ctx.enter_context(tc.manual_schedule())
 
         k_sb = keep.tile([P, NKV, QT, HD], BF16)
-        q_sb = keep.tile([P, QT, NH, HD], BF16)
+        q_sb = keep.tile([P, 2, NH, 2, HD], BF16)
         v_sb = keep.tile([P, NKV, 4, HD], BF16)
         vp_sb = keep.tile([P, NKV, 4, HD], BF16)
         wo_sb = keep.tile([P, D // P, D], BF16)
 
-        def load_q(i, h0, h1):
+        def load_k(g):
+            nc.sync.dma_start(out=k_sb[:, g], in_=k_rot[0, g].rearrange("(t p) d -> p t d", p=P))
+
+        def load_q(h, g):
+            heads = slice(g * REP, (g + 1) * REP)
             nc.sync.dma_start(
-                out=q_sb[:, i, h0:h1, :], in_=q_rot[0, h0:h1, i * P : (i + 1) * P, :].rearrange("h p d -> p h d")
+                out=q_sb[:, h, heads].rearrange("p a j d -> p a (j d)"),
+                in_=q_rot[0, heads, 256 * h : 256 * (h + 1), :].rearrange("a (p j) d -> p a (j d)", j=2),
             )
 
         def load_wo(c):
@@ -74,33 +81,23 @@ def tile_rlaattention_pb_kernel(tc, q_rot, k_rot, v, Wo, out):
                 in_=Wo[256 * c : 256 * (c + 1), :].rearrange("(b p) k -> p b k", p=P),
             )
 
-        def load_k_and_first_q(g):
-            nc.sync.dma_start(out=k_sb[:, g], in_=k_rot[0, g].rearrange("(t p) d -> p t d", p=P))
-            load_q(0, g * REP, (g + 1) * REP)
-
-        load_k_and_first_q(0)
-        load_k_and_first_q(1)
-        for c in range(2):
-            for u in range(2):
-                nc.sync.dma_start(
-                    out=vp_sb[64 * c : 64 * (c + 1), :, 2 * u : 2 * u + 2, :].rearrange("w g e d -> w g (e d)"),
-                    in_=v[0, :, P * u : P * (u + 1), :].rearrange("g (w e) d -> w g (e d)", e=2),
-                )
-        load_k_and_first_q(2)
-        load_wo(0)
-        load_k_and_first_q(3)
-        load_wo(1)
-        load_q(1, 0, NH)
-        for c in range(2, 5):
+        for g in range(NKV):
+            load_k(g)
+            load_q(0, g)
+            if g == 1:
+                for c in range(2):
+                    nc.sync.dma_start(
+                        out=vp_sb[64 * c : 64 * (c + 1)].rearrange("w g t d -> w g (t d)"),
+                        in_=v[0, :, 0 : S // 2, :].rearrange("g (w t) d -> w g (t d)", t=4),
+                    )
+        for c in range(8):
             load_wo(c)
-        load_q(2, 0, NH)
-        for c in range(5, 8):
-            load_wo(c)
+        load_q(1, 0)
         nc.sync.dma_start(
-            out=v_sb[:].rearrange("p g (u e) d -> p (g u) (e d)", u=2),
-            in_=v[0].rearrange("g (u p e) d -> p (g u) (e d)", u=2, p=P, e=2),
+            out=v_sb[:].rearrange("p g t d -> p g (t d)"), in_=v[0].rearrange("g (p t) d -> p g (t d)", t=4)
         )
-        load_q(3, 0, NH)
+        for g in range(1, NKV):
+            load_q(1, g)
 
         ident_bf = const.tile([P, P], BF16)
         make_identity(nc, ident_bf[:])
@@ -121,14 +118,23 @@ def tile_rlaattention_pb_kernel(tc, q_rot, k_rot, v, Wo, out):
         e_wide = [keep.tile([P, S], BF16, name="e_wide%d" % slot) for slot in range(2 * REP)]
         e_pair = [keep.tile([P, S], BF16, name="e_pair%d" % slot) for slot in range(REP)]
         for e_tile in e_wide:
-            nc.vector.memset(e_tile[:, 3 * P : S], 0.0)
+            nc.vector.memset(e_tile[:].rearrange("p (u k) -> p u k", u=2)[:, :, 3 * P // 2 :], 0.0)
         for e_tile in e_pair:
-            nc.vector.memset(e_tile[:, 2 * P : S], 0.0)
+            nc.vector.memset(e_tile[:].rearrange("p (u c k) -> p u c k", u=2, c=2)[:, :, :, P // 2 :], 0.0)
         mask_bf = const.tile([P, P], BF16)
         nc.vector.tensor_copy(out=mask_bf[:], in_=mask_f32[:])
 
+        order_rows = const.tile([P, P], BF16)
+        nc.vector.tensor_copy(
+            out=order_rows[:].rearrange("p (j w) -> p j w", j=2), in_=ident_bf[:].rearrange("p (w j) -> p j w", j=2)
+        )
+        order_queries = const.tile([P, P], F32)
+        nc.vector.tensor_copy(
+            out=order_queries[:].rearrange("p (w j) -> p w j", j=2), in_=ident_f32[:].rearrange("p (j w) -> p w j", j=2)
+        )
+
         kT = keep.tile([P, NKV, S], BF16)
-        qT = keep.tile([P, UNITS, REP, P], BF16)
+        qT = keep.tile([P, 2 * NKV, 2, REP, P], BF16)
         v_codes = keep.tile([P, NKV * HD], U32, align_bytes=64)
         v_scales = keep.tile([P, NKV * HD], U8, align_bytes=64)
         vd_codes = keep.tile([P, NKV * HD], U32, align_bytes=64)
@@ -158,28 +164,39 @@ def tile_rlaattention_pb_kernel(tc, q_rot, k_rot, v, Wo, out):
             kt_ps = psum.tile([P, QT, P], BF16, tag="x")
             for t in range(QT):
                 nc.tensor.transpose(kt_ps[:, t, :], k_sb[:, g, t, :], ident_bf[:])
-            nc.vector.tensor_copy(out=kT[:, g, :], in_=kt_ps[:].rearrange("p t k -> p (t k)"))
+            nc.scalar.copy(out=kT[:, g, :], in_=kt_ps[:].rearrange("p t k -> p (t k)"))
 
-        def transpose_q(n):
-            if not is_unit(n):
-                return
-            i, g = divmod(n, NKV)
-            qt_ps = psum.tile([P, REP, P], BF16, tag="x")
+        def transpose_q(m):
+            h, g = divmod(m, NKV)
+            qt_ps = psum.tile([P, REP, 2, P], BF16, tag="x")
             for a in range(REP):
-                nc.tensor.transpose(qt_ps[:, a, :], q_sb[:, i, g * REP + a, :], ident_bf[:])
-            live["qT", n] = qt_ps
+                for j in range(2):
+                    nc.tensor.transpose(qt_ps[:, a, j, :], q_sb[:, h, g * REP + a, j, :], ident_bf[:])
+            live["qT", m] = qt_ps
 
-        def copy_qT(n):
-            if is_unit(n):
-                nc.scalar.copy(out=qT[:, n], in_=live["qT", n][:])
+        def copy_qT(m):
+            tiles = live["qT", m][:].rearrange("p a j (i w) -> p i (a j) w", i=2)
+            for i in range(2):
+                nc.scalar.copy(out=qT[:, m, i].rearrange("p a (j w) -> p (a j) w", j=2), in_=tiles[:, i])
 
-        def group_v(source):
-            v_grouped = work.tile([P, N_TILE * 4], BF16, align_bytes=64, bufs=1)
+        def group_vp():
+            live["vp"] = work.tile([P, N_TILE * 4], BF16, align_bytes=64, bufs=1, name="v_grouped")
             nc.vector.tensor_copy(
-                out=v_grouped[:].rearrange("p (g d t) -> p g d t", g=NKV, t=4),
-                in_=source[:].rearrange("p g t d -> p g d t"),
+                out=live["vp"][:].rearrange("p (g d t) -> p g d t", g=NKV, t=4),
+                in_=vp_sb[:].rearrange("p g t d -> p g d t"),
             )
-            return v_grouped
+
+        def group_v(g):
+            if g == 0:
+                live["v"] = work.tile([P, N_TILE * 4], BF16, align_bytes=64, bufs=1, name="v_grouped")
+            nc.gpsimd.tensor_scalar(
+                out=live["v"][:].rearrange("p (g d t) -> p g d t", g=NKV, t=4)[:, g],
+                in0=v_sb[:, g].rearrange("p t d -> p d t"),
+                scalar1=1.0,
+                scalar2=0.0,
+                op0=ALU.mult,
+                op1=ALU.add,
+            )
 
         def quantise_v(v_grouped, codes, scales):
             nc.vector.quantize_mx(out=codes[:].bitcast(FP8X4), scales=scales[:], in_=v_grouped[:])
@@ -202,6 +219,7 @@ def tile_rlaattention_pb_kernel(tc, q_rot, k_rot, v, Wo, out):
             n, a0 = divmod(k, REP)
             i, g = divmod(n, NKV)
             width = (i + 1) * P
+            queries = qT[:, (i // 2) * NKV + g, i % 2]
             s_ps = psum.tile([P, BANK], F32, tag="s")
             live["s", k] = s_ps
             for c in range(heads_per_bank(n)):
@@ -209,14 +227,14 @@ def tile_rlaattention_pb_kernel(tc, q_rot, k_rot, v, Wo, out):
                 diag = lo + i * P
                 if i > 0:
                     nc.tensor.matmul(
-                        out=s_ps[:, lo:diag], lhsT=qT[:, n, a0 + c, :], rhs=kT[:, g, 0 : i * P], start=True, stop=True
+                        out=s_ps[:, lo:diag], lhsT=queries[:, a0 + c, :], rhs=kT[:, g, 0 : i * P], start=True, stop=True
                     )
                 nc.tensor.matmul(
-                    out=s_ps[:, diag : diag + P], lhsT=ident_bf[:], rhs=mask_bf[:], start=True, stop=False
+                    out=s_ps[:, diag : diag + P], lhsT=order_rows[:], rhs=mask_bf[:], start=True, stop=False
                 )
                 nc.tensor.matmul(
                     out=s_ps[:, diag : diag + P],
-                    lhsT=qT[:, n, a0 + c, :],
+                    lhsT=queries[:, a0 + c, :],
                     rhs=kT[:, g, i * P : (i + 1) * P],
                     start=False,
                     stop=True,
@@ -254,13 +272,14 @@ def tile_rlaattention_pb_kernel(tc, q_rot, k_rot, v, Wo, out):
             width = (n // NKV + 1) * P
             c = a % heads_per_bank(n)
             if n < NARROW:
-                pair = e_pair[(n % 2) * 2 + a // 2][:].rearrange("p (u c k) -> p u c k", u=2, c=2)
-                e_out = pair[:, 0 : width // P, a % 2, :]
+                pair = e_pair[(n % 2) * 2 + a // 2][:].rearrange("p (u c w e) -> p u c w e", u=2, c=2, e=2)
+                e_out = pair[:, :, a % 2, 0 : width // 4, :]
             else:
-                e_out = e_wide[(n % 2) * REP + a][:, 0:width].rearrange("p (u k) -> p u k", k=P)
+                e_tile = e_wide[(n % 2) * REP + a]
+                e_out = e_tile[:].rearrange("p (u w e) -> p u w e", u=2, e=2)[:, :, 0 : width // 4, :]
             nc.scalar.activation(
                 out=e_out,
-                in_=live["s", k - c][:, c * width : (c + 1) * width].rearrange("p (u k) -> p u k", k=P),
+                in_=live["s", k - c][:, c * width : (c + 1) * width].rearrange("p (w u e) -> p u w e", u=2, e=2),
                 func=ACT.Exp,
                 bias=live["neg", n][:, a : a + 1],
                 scale=SCALE,
@@ -292,7 +311,8 @@ def tile_rlaattention_pb_kernel(tc, q_rot, k_rot, v, Wo, out):
             words = e_grouped[:].bitcast(F32).rearrange("p (a q u) -> p a q u", a=REP, u=2)
             nc.scalar.copy(out=words[:, 0:2], in_=live["eT", n, 0][:].rearrange("p c u q -> p c q u"))
             if n >= NARROW:
-                nc.vector.tensor_copy(out=words[:, 2:4], in_=live["eT", n, 1][:].rearrange("p c u q -> p c q u"))
+                copy = nc.scalar.copy if n % 2 else nc.vector.tensor_copy
+                copy(out=words[:, 2:4], in_=live["eT", n, 1][:].rearrange("p c u q -> p c q u"))
 
         def quantise_e(n):
             if not is_unit(n):
@@ -345,7 +365,7 @@ def tile_rlaattention_pb_kernel(tc, q_rot, k_rot, v, Wo, out):
             ot_ps = psum.tile([P, 2, P], F32, tag="x")
             live["oT", n] = ot_ps
             for u in range(2):
-                nc.tensor.transpose(ot_ps[:, u, :], o_words[:, u * P : (u + 1) * P], ident_f32[:])
+                nc.tensor.transpose(ot_ps[:, u, :], o_words[:, u * P : (u + 1) * P], order_queries[:])
 
         def copy_oT(n):
             if not is_unit(n):
@@ -420,18 +440,26 @@ def tile_rlaattention_pb_kernel(tc, q_rot, k_rot, v, Wo, out):
             for g in range(PASSES):
                 project_pass(f_ps, i, nt, g)
 
+        def wo_upto(beat):
+            return min(WO_BANKS, sum(WO_PER_BEAT[b % REP] for b in range(WO_FIRST_BEAT, beat + 1)))
+
+        def wo_banks(beat):
+            return range(wo_upto(beat - 1), wo_upto(beat))
+
         def project_beats():
             beats = {}
-            free = 0
+            beat = 0
             for job in range(3 * NT):
                 i, nt = divmod(job, NT)
-                wo_ready = WO_FIRST_BEAT + (WO_BANKS // NT) * (nt + 1) + QUANTISE_WO
                 o_ready = REP * (NKV * i + NKV - 1) + QUANTISE_O + 1
-                beat = max(wo_ready, o_ready, free)
-                while beat % REP != 1:
+                while (
+                    beat % REP != 1
+                    or beat < o_ready
+                    or wo_upto(beat - 1 - QUANTISE_WO) < (WO_BANKS // NT) * (nt + 1)
+                ):
                     beat += 1
                 beats[beat] = job
-                free = beat + REP
+                beat += 1
             return beats
 
         def project_last(g):
@@ -446,10 +474,14 @@ def tile_rlaattention_pb_kernel(tc, q_rot, k_rot, v, Wo, out):
             n, rest = divmod(beat - delay, REP)
             return n if rest == 0 and is_unit(n) else -1
 
+        def q_beat(m):
+            h, g = divmod(m, NKV)
+            return SECOND_Q + SECOND_Q_STEP * g if h else max(REP * g + TRANSPOSE_Q, -SCORES_AHEAD)
+
         transpose_k(0)
         transpose_q(0)
         copy_qT(0)
-        for beat in range(-SCORES_AHEAD, BEATS + QUANTISE_O):
+        for beat in range(-SCORES_AHEAD, REP * (UNITS - 1) + QUANTISE_O + 1):
             quantise_o(due(beat, QUANTISE_O))
             copy_oT(due(beat, COPY_O))
             transpose_o(due(beat, TRANSPOSE_O))
@@ -468,27 +500,32 @@ def tile_rlaattention_pb_kernel(tc, q_rot, k_rot, v, Wo, out):
                 if not last:
                     last.extend(psum.tile([P, N_TILE], F32, tag="s", name="last%d" % nt) for nt in range(NT))
                 project_last(last_passes[beat])
-            for n in range(1, UNITS):
-                if max(REP * n + COPY_Q, -SCORES_AHEAD) == beat:
-                    copy_qT(n)
-                if max(REP * n + TRANSPOSE_Q, -SCORES_AHEAD) == beat:
-                    transpose_k(n)
-                    transpose_q(n)
+            for m in range(1, 2 * NKV):
+                if beat == q_beat(m) + 1:
+                    copy_qT(m)
+                if beat == q_beat(m):
+                    if m < NKV:
+                        transpose_k(m)
+                    transpose_q(m)
             if beat - 1 in jobs:
                 job = jobs[beat - 1]
                 store(live["f", job], job // NT, job % NT, nc.scalar.copy)
-            copy_woT(beat - WO_FIRST_BEAT - COPY_WO)
-            quantise_wo(beat - WO_FIRST_BEAT - QUANTISE_WO)
-            transpose_wo(beat - WO_FIRST_BEAT)
-            if beat == QUANTISE_VP:
-                vp_grouped = group_v(vp_sb)
-            if beat == QUANTISE_VP + 1:
-                quantise_v(vp_grouped, vd_codes, vd_scales)
-            if beat == QUANTISE_VP + 2:
+            for f in wo_banks(beat - COPY_WO):
+                copy_woT(f)
+            for f in wo_banks(beat - QUANTISE_WO):
+                quantise_wo(f)
+            for f in wo_banks(beat):
+                transpose_wo(f)
+            if beat == PREPARE_VP:
+                group_vp()
+            if beat == PREPARE_VP + 1:
+                quantise_v(live["vp"], vd_codes, vd_scales)
+            if beat == PREPARE_VP + 2:
                 spread_v_pair()
-            if beat == QUANTISE_V:
-                quantise_v(group_v(v_sb), v_codes, v_scales)
-        quantise_o(UNITS - 1)
+            if 0 <= beat - PREPARE_V < NKV:
+                group_v(beat - PREPARE_V)
+            if beat == PREPARE_V + 6:
+                quantise_v(live["v"], v_codes, v_scales)
         project_last(PASSES - 1)
         for nt in range(NT):
             store(last[nt], QT - 1, nt, nc.vector.tensor_copy if nt % 2 else nc.scalar.copy)

@@ -56,7 +56,7 @@ def tile_rlaattention_pb_kernel(tc, q_rot, k_rot, v, Wo, out):
         keep = ctx.enter_context(tc.tile_pool(name="keep", bufs=1))
         work = ctx.enter_context(tc.tile_pool(name="work", bufs=3))
         stat = ctx.enter_context(tc.tile_pool(name="stat", bufs=6))
-        psum = ctx.enter_context(tc.psum_pool(name="psum", bufs=4))
+        psum = ctx.enter_context(tc.psum_pool(name="psum", bufs=8))
         ctx.enter_context(tc.manual_schedule())
 
         k_sb = keep.tile([P, NKV, QT, HD], BF16)
@@ -161,14 +161,14 @@ def tile_rlaattention_pb_kernel(tc, q_rot, k_rot, v, Wo, out):
         def transpose_k(g):
             if g >= NKV:
                 return
-            kt_ps = psum.tile([P, QT, P], BF16, tag="x")
+            kt_ps = psum.tile([P, QT, P], BF16, tag="bank")
             for t in range(QT):
                 nc.tensor.transpose(kt_ps[:, t, :], k_sb[:, g, t, :], ident_bf[:])
             nc.scalar.copy(out=kT[:, g, :], in_=kt_ps[:].rearrange("p t k -> p (t k)"))
 
         def transpose_q(m):
             h, g = divmod(m, NKV)
-            qt_ps = psum.tile([P, REP, 2, P], BF16, tag="x")
+            qt_ps = psum.tile([P, REP, 2, P], BF16, tag="bank")
             for a in range(REP):
                 for j in range(2):
                     nc.tensor.transpose(qt_ps[:, a, j, :], q_sb[:, h, g * REP + a, j, :], ident_bf[:])
@@ -220,7 +220,7 @@ def tile_rlaattention_pb_kernel(tc, q_rot, k_rot, v, Wo, out):
             i, g = divmod(n, NKV)
             width = (i + 1) * P
             queries = qT[:, (i // 2) * NKV + g, i % 2]
-            s_ps = psum.tile([P, BANK], F32, tag="s")
+            s_ps = psum.tile([P, BANK], F32, tag="bank")
             live["s", k] = s_ps
             for c in range(heads_per_bank(n)):
                 lo = c * width
@@ -296,7 +296,7 @@ def tile_rlaattention_pb_kernel(tc, q_rot, k_rot, v, Wo, out):
                 return
             tiles = e_pair[(n % 2) * 2 : (n % 2) * 2 + 2] if n < NARROW else e_wide[(n % 2) * REP : (n % 2 + 1) * REP]
             for half in range(len(tiles) // 2):
-                et_ps = psum.tile([P, 2, 2, P], F32, tag="x")
+                et_ps = psum.tile([P, 2, 2, P], F32, tag="bank")
                 live["eT", n, half] = et_ps
                 for c in range(2):
                     e_words = tiles[2 * half + c][:].bitcast(F32)
@@ -332,7 +332,7 @@ def tile_rlaattention_pb_kernel(tc, q_rot, k_rot, v, Wo, out):
             if not is_unit(n):
                 return
             g = n % NKV
-            o_ps = psum.tile([P, REP * HD], F32, tag="x")
+            o_ps = psum.tile([P, REP * HD], F32, tag="bank")
             live["o", n] = o_ps
             codes, scales, width = (vp_codes, vp_scales, 2 * HD) if n < NARROW else (v_codes, v_scales, HD)
             for m in range(REP * HD // width):
@@ -362,7 +362,7 @@ def tile_rlaattention_pb_kernel(tc, q_rot, k_rot, v, Wo, out):
             if not is_unit(n):
                 return
             o_words = live["o_sb", n][:].bitcast(F32)
-            ot_ps = psum.tile([P, 2, P], F32, tag="x")
+            ot_ps = psum.tile([P, 2, P], F32, tag="bank")
             live["oT", n] = ot_ps
             for u in range(2):
                 nc.tensor.transpose(ot_ps[:, u, :], o_words[:, u * P : (u + 1) * P], order_queries[:])
@@ -387,7 +387,7 @@ def tile_rlaattention_pb_kernel(tc, q_rot, k_rot, v, Wo, out):
             if not 0 <= f < WO_BANKS:
                 return
             c, g = divmod(f, PASSES)
-            wt_ps = psum.tile([P, 2, 2, P], F32, tag="x")
+            wt_ps = psum.tile([P, 2, 2, P], F32, tag="bank")
             live["wT", f] = wt_ps
             for b in range(2):
                 w_words = wo_sb[:, 2 * c + b, :].bitcast(F32)
@@ -435,7 +435,7 @@ def tile_rlaattention_pb_kernel(tc, q_rot, k_rot, v, Wo, out):
 
         def project(job):
             i, nt = divmod(job, NT)
-            f_ps = psum.tile([P, N_TILE], F32, tag="x")
+            f_ps = psum.tile([P, N_TILE], F32, tag="bank")
             live["f", job] = f_ps
             for g in range(PASSES):
                 project_pass(f_ps, i, nt, g)
@@ -453,7 +453,7 @@ def tile_rlaattention_pb_kernel(tc, q_rot, k_rot, v, Wo, out):
                 i, nt = divmod(job, NT)
                 o_ready = REP * (NKV * i + NKV - 1) + QUANTISE_O + 1
                 while (
-                    beat % REP != 1
+                    beat % REP != 2
                     or beat < o_ready
                     or wo_upto(beat - 1 - QUANTISE_WO) < (WO_BANKS // NT) * (nt + 1)
                 ):
@@ -484,7 +484,6 @@ def tile_rlaattention_pb_kernel(tc, q_rot, k_rot, v, Wo, out):
         for beat in range(-SCORES_AHEAD, REP * (UNITS - 1) + QUANTISE_O + 1):
             quantise_o(due(beat, QUANTISE_O))
             copy_oT(due(beat, COPY_O))
-            transpose_o(due(beat, TRANSPOSE_O))
             scale_o(due(beat, SCALE_O))
             e_times_v(due(beat, TIMES_V))
             quantise_e(due(beat, QUANTISE_E))
@@ -492,13 +491,14 @@ def tile_rlaattention_pb_kernel(tc, q_rot, k_rot, v, Wo, out):
             transpose_e(due(beat, TRANSPOSE_E))
             exp_head(beat)
             scores(beat + SCORES_AHEAD)
+            transpose_o(due(beat, TRANSPOSE_O))
             row_max(beat + MAX_AHEAD)
             reciprocal(due(beat, COPY_E))
             if beat in jobs:
                 project(jobs[beat])
             if beat in last_passes:
                 if not last:
-                    last.extend(psum.tile([P, N_TILE], F32, tag="s", name="last%d" % nt) for nt in range(NT))
+                    last.extend(psum.tile([P, N_TILE], F32, tag="bank", name="last%d" % nt) for nt in range(NT))
                 project_last(last_passes[beat])
             for m in range(1, 2 * NKV):
                 if beat == q_beat(m) + 1:

@@ -35,7 +35,7 @@ BEATS = UNITS * REP
 WO_ROWS = 256
 WO_BANKS = D // WO_ROWS * PASSES
 WO_FIRST_BEAT = 8
-WO_PER_BEAT = (1, 1, 2, 1)
+WO_PER_BEAT = (1, 1, 1, 2)
 
 TRANSPOSE_Q = -6
 SCORES_AHEAD, MAX_AHEAD = 3, 2
@@ -43,7 +43,7 @@ TRANSPOSE_E, COPY_E, QUANTISE_E, TIMES_V = 4, 5, 6, 7
 SCALE_O, TRANSPOSE_O, COPY_O, QUANTISE_O = 8, 9, 10, 11
 COPY_WO, QUANTISE_WO = 1, 3
 PREPARE_VP, PREPARE_V = 1, 28
-SECOND_Q, SECOND_Q_STEP = 25, 3
+SECOND_Q = 25
 NARROW = 2 * NKV
 
 FLOPS = 2 * NH * S * S * HD * 2 + 2 * S * D * D
@@ -398,7 +398,7 @@ def tile_rlaattention_pb_kernel(tc, q_rot, k_rot, v, Wo, out):
         def copy_woT(f):
             if not 0 <= f < WO_BANKS:
                 return
-            w_grouped = work.tile([P, WO_ROWS * 4], BF16, align_bytes=64, bufs=4)
+            w_grouped = work.tile([P, WO_ROWS * 4], BF16, align_bytes=64, bufs=5)
             live["w_grouped", f] = w_grouped
             words = w_grouped[:].bitcast(F32).rearrange("p (b n u) -> p b n u", b=2, u=2)
             source = live["wT", f][:].rearrange("p b u n -> p b n u")
@@ -452,8 +452,9 @@ def tile_rlaattention_pb_kernel(tc, q_rot, k_rot, v, Wo, out):
             for job in range(3 * NT):
                 i, nt = divmod(job, NT)
                 o_ready = REP * (NKV * i + NKV - 1) + QUANTISE_O + 1
+                step = 2 if i == 2 and nt > 0 else REP
                 while (
-                    beat % REP != 2
+                    beat % step != 2 % step
                     or beat < o_ready
                     or wo_upto(beat - 1 - QUANTISE_WO) < (WO_BANKS // NT) * (nt + 1)
                 ):
@@ -476,7 +477,7 @@ def tile_rlaattention_pb_kernel(tc, q_rot, k_rot, v, Wo, out):
 
         def q_beat(m):
             h, g = divmod(m, NKV)
-            return SECOND_Q + SECOND_Q_STEP * g if h else max(REP * g + TRANSPOSE_Q, -SCORES_AHEAD)
+            return SECOND_Q + REP * g if h else max(REP * g + TRANSPOSE_Q, -SCORES_AHEAD)
 
         transpose_k(0)
         transpose_q(0)
@@ -494,12 +495,6 @@ def tile_rlaattention_pb_kernel(tc, q_rot, k_rot, v, Wo, out):
             transpose_o(due(beat, TRANSPOSE_O))
             row_max(beat + MAX_AHEAD)
             reciprocal(due(beat, COPY_E))
-            if beat in jobs:
-                project(jobs[beat])
-            if beat in last_passes:
-                if not last:
-                    last.extend(psum.tile([P, N_TILE], F32, tag="bank", name="last%d" % nt) for nt in range(NT))
-                project_last(last_passes[beat])
             for m in range(1, 2 * NKV):
                 if beat == q_beat(m) + 1:
                     copy_qT(m)
@@ -526,6 +521,12 @@ def tile_rlaattention_pb_kernel(tc, q_rot, k_rot, v, Wo, out):
                 group_v(beat - PREPARE_V)
             if beat == PREPARE_V + 6:
                 quantise_v(live["v"], v_codes, v_scales)
+            if beat in jobs:
+                project(jobs[beat])
+            if beat in last_passes:
+                if not last:
+                    last.extend(psum.tile([P, N_TILE], F32, tag="bank", name="last%d" % nt) for nt in range(NT))
+                project_last(last_passes[beat])
         project_last(PASSES - 1)
         for nt in range(NT):
             store(last[nt], QT - 1, nt, nc.vector.tensor_copy if nt % 2 else nc.scalar.copy)

@@ -135,17 +135,17 @@ def tile_rlaattention_pb_kernel(tc, q_rot, k_rot, v, Wo, out):
 
         kT = keep.tile([P, NKV, S], BF16)
         qT = keep.tile([P, 2 * NKV, 2, REP, P], BF16)
-        v_codes = keep.tile([P, NKV * HD], U32, align_bytes=64)
-        v_scales = keep.tile([P, NKV * HD], U8, align_bytes=64)
-        vd_codes = keep.tile([P, NKV * HD], U32, align_bytes=64)
-        vd_scales = keep.tile([P, NKV * HD], U8, align_bytes=64)
-        vp_codes = keep.tile([P, NKV * 2 * HD], U32, align_bytes=64)
+        v_codes = keep.tile([P, NKV * HD], U32, align_bytes=256)
+        v_scales = keep.tile([P, NKV * HD], U8, align_bytes=256)
+        vd_codes = keep.tile([P, NKV * HD], U32, align_bytes=256)
+        vd_scales = keep.tile([P, NKV * HD], U8, align_bytes=256)
+        vp_codes = keep.tile([P, NKV * 2 * HD], U32, align_bytes=256)
         nc.vector.memset(vp_codes[:].bitcast(I32), 0)
-        vp_scales = keep.tile([P, NKV * 2 * HD], U8, align_bytes=64)
-        w_codes = keep.tile([P, PASSES, D], U32, align_bytes=64)
-        w_scales = keep.tile([P, PASSES, D], U8, align_bytes=64)
-        o_codes = keep.tile([P, UNITS, P], U32, align_bytes=64)
-        o_scales = keep.tile([P, UNITS, P], U8, align_bytes=64)
+        vp_scales = keep.tile([P, NKV * 2 * HD], U8, align_bytes=256)
+        w_codes = keep.tile([P, PASSES, D], U32, align_bytes=256)
+        w_scales = keep.tile([P, PASSES, D], U8, align_bytes=256)
+        o_codes = keep.tile([P, UNITS, P], U32, align_bytes=256)
+        o_scales = keep.tile([P, UNITS, P], U8, align_bytes=256)
 
         live = {}
 
@@ -317,8 +317,8 @@ def tile_rlaattention_pb_kernel(tc, q_rot, k_rot, v, Wo, out):
         def quantise_e(n):
             if not is_unit(n):
                 return
-            e_codes = work.tile([P, REP * P], U32, align_bytes=64)
-            e_scales = work.tile([P, REP * P], U8, align_bytes=64)
+            e_codes = work.tile([P, REP * P], U32, align_bytes=256)
+            e_scales = work.tile([P, REP * P], U8, align_bytes=256)
             live["e_codes", n] = e_codes
             live["e_scales", n] = e_scales
             count = (2 if n < NARROW else REP) * P
@@ -490,6 +490,8 @@ def tile_rlaattention_pb_kernel(tc, q_rot, k_rot, v, Wo, out):
             quantise_e(due(beat, QUANTISE_E))
             copy_eT(due(beat, COPY_E))
             transpose_e(due(beat, TRANSPOSE_E))
+            for f in wo_banks(beat - QUANTISE_WO):
+                quantise_wo(f)
             exp_head(beat)
             scores(beat + SCORES_AHEAD)
             transpose_o(due(beat, TRANSPOSE_O))
@@ -507,8 +509,6 @@ def tile_rlaattention_pb_kernel(tc, q_rot, k_rot, v, Wo, out):
                 store(live["f", job], job // NT, job % NT, nc.scalar.copy)
             for f in wo_banks(beat - COPY_WO):
                 copy_woT(f)
-            for f in wo_banks(beat - QUANTISE_WO):
-                quantise_wo(f)
             for f in wo_banks(beat):
                 transpose_wo(f)
             if beat == PREPARE_VP:

from contextlib import ExitStack
import math

import concourse.mybir as mybir
from concourse.masks import make_identity

BF16 = mybir.dt.bfloat16
F32 = mybir.dt.float32
U32 = mybir.dt.uint32
U8 = mybir.dt.uint8
I32 = mybir.dt.int32
FP8X4 = mybir.dt.float8_e4m3fn_x4
ACT = mybir.ActivationFunctionType
ALU = mybir.AluOpType
AXIS = mybir.AxisListType

P = 128
S = 512
HD = 128
NH = 16
NKV = 4
REP = NH // NKV
D = 2048
QT = S // P
K_PASS = 512
PASSES = D // K_PASS
N_TILE = 512
NT = D // N_TILE
BANK = 512
SCALE = 1.0 / math.sqrt(HD)
NEG = -1.0e30

UNITS = QT * NKV
BEATS = UNITS * REP
WO_ROWS = 256
WO_BANKS = D // WO_ROWS * PASSES
WO_FIRST_BEAT = 8
WO_PER_BEAT = (1, 1, 1, 2)

TRANSPOSE_Q = -6
SCORES_AHEAD, MAX_AHEAD = 3, 2
TRANSPOSE_E, COPY_E, QUANTISE_E, TIMES_V = 4, 5, 6, 7
SCALE_O, TRANSPOSE_O, COPY_O, QUANTISE_O = 8, 9, 10, 11
COPY_WO, QUANTISE_WO = 1, 3
PREPARE_VP, PREPARE_V = 1, 28
SECOND_Q = 25
NARROW = 2 * NKV

FLOPS = 2 * NH * S * S * HD * 2 + 2 * S * D * D


def tile_rlaattention_pb_kernel(tc, q_rot, k_rot, v, Wo, out):
    nc = tc.nc
    with ExitStack() as ctx:
        const = ctx.enter_context(tc.tile_pool(name="const", bufs=1))
        keep = ctx.enter_context(tc.tile_pool(name="keep", bufs=1))
        work = ctx.enter_context(tc.tile_pool(name="work", bufs=3))
        stat = ctx.enter_context(tc.tile_pool(name="stat", bufs=6))
        psum = ctx.enter_context(tc.psum_pool(name="psum", bufs=8))
        ctx.enter_context(tc.manual_schedule())

        k_sb = keep.tile([P, NKV, QT, HD], BF16)
        q_sb = keep.tile([P, 2, NH, 2, HD], BF16)
        v_sb = keep.tile([P, NKV, 4, HD], BF16)
        vp_sb = keep.tile([P, NKV, 4, HD], BF16)
        wo_sb = keep.tile([P, D // P, D], BF16)

        def load_k(g):
            nc.sync.dma_start(out=k_sb[:, g], in_=k_rot[0, g].rearrange("(t p) d -> p t d", p=P))

        def load_q(h, g):
            heads = slice(g * REP, (g + 1) * REP)
            nc.sync.dma_start(
                out=q_sb[:, h, heads].rearrange("p a j d -> p a (j d)"),
                in_=q_rot[0, heads, 256 * h : 256 * (h + 1), :].rearrange("a (p j) d -> p a (j d)", j=2),
            )

        def load_wo(c):
            nc.sync.dma_start(
                out=wo_sb[:, 2 * c : 2 * c + 2, :],
                in_=Wo[256 * c : 256 * (c + 1), :].rearrange("(b p) k -> p b k", p=P),
            )

        for g in range(NKV):
            load_k(g)
            load_q(0, g)
            if g == 1:
                for c in range(2):
                    nc.sync.dma_start(
                        out=vp_sb[64 * c : 64 * (c + 1)].rearrange("w g t d -> w g (t d)"),
                        in_=v[0, :, 0 : S // 2, :].rearrange("g (w t) d -> w g (t d)", t=4),
                    )
        for c in range(8):
            load_wo(c)
        load_q(1, 0)
        nc.sync.dma_start(
            out=v_sb[:].rearrange("p g t d -> p g (t d)"), in_=v[0].rearrange("g (p t) d -> p g (t d)", t=4)
        )
        for g in range(1, NKV):
            load_q(1, g)

        ident_bf = const.tile([P, P], BF16)
        make_identity(nc, ident_bf[:])
        ident_f32 = const.tile([P, P], F32)
        make_identity(nc, ident_f32[:])
        mask_f32 = const.tile([P, P], F32)
        nc.gpsimd.memset(mask_f32[:], 0.0)
        nc.gpsimd.affine_select(
            out=mask_f32[:],
            in_=mask_f32[:],
            pattern=[[-1, P]],
            compare_op=ALU.is_ge,
            fill=NEG,
            base=0,
            channel_multiplier=1,
        )

        e_wide = [keep.tile([P, S], BF16, name="e_wide%d" % slot) for slot in range(2 * REP)]
        e_pair = [keep.tile([P, S], BF16, name="e_pair%d" % slot) for slot in range(REP)]
        for e_tile in e_wide:
            nc.vector.memset(e_tile[:].rearrange("p (u k) -> p u k", u=2)[:, :, 3 * P // 2 :], 0.0)
        for e_tile in e_pair:
            nc.vector.memset(e_tile[:].rearrange("p (u c k) -> p u c k", u=2, c=2)[:, :, :, P // 2 :], 0.0)
        mask_bf = const.tile([P, P], BF16)
        nc.vector.tensor_copy(out=mask_bf[:], in_=mask_f32[:])

        order_rows = const.tile([P, P], BF16)
        nc.vector.tensor_copy(
            out=order_rows[:].rearrange("p (j w) -> p j w", j=2), in_=ident_bf[:].rearrange("p (w j) -> p j w", j=2)
        )
        order_queries = const.tile([P, P], F32)
        nc.vector.tensor_copy(
            out=order_queries[:].rearrange("p (w j) -> p w j", j=2), in_=ident_f32[:].rearrange("p (j w) -> p w j", j=2)
        )

        kT = keep.tile([P, NKV, S], BF16)
        qT = keep.tile([P, 2 * NKV, 2, REP, P], BF16)
        v_codes = keep.tile([P, NKV * HD], U32, align_bytes=256)
        v_scales = keep.tile([P, NKV * HD], U8, align_bytes=256)
        vd_codes = keep.tile([P, NKV * HD], U32, align_bytes=256)
        vd_scales = keep.tile([P, NKV * HD], U8, align_bytes=256)
        vp_codes = keep.tile([P, NKV * 2 * HD], U32, align_bytes=256)
        nc.vector.memset(vp_codes[:].bitcast(I32), 0)
        vp_scales = keep.tile([P, NKV * 2 * HD], U8, align_bytes=256)
        w_codes = keep.tile([P, PASSES, D], U32, align_bytes=256)
        w_scales = keep.tile([P, PASSES, D], U8, align_bytes=256)
        o_codes = keep.tile([P, UNITS, P], U32, align_bytes=256)
        o_scales = keep.tile([P, UNITS, P], U8, align_bytes=256)

        live = {}

        def is_unit(n):
            return 0 <= n < UNITS

        def heads_per_bank(n):
            return BANK // ((n // NKV + 1) * P)

        def opens_bank(k):
            return 0 <= k < BEATS and (k % REP) % heads_per_bank(k // REP) == 0

        def transpose_k(g):
            if g >= NKV:
                return
            kt_ps = psum.tile([P, QT, P], BF16, tag="bank")
            for t in range(QT):
                nc.tensor.transpose(kt_ps[:, t, :], k_sb[:, g, t, :], ident_bf[:])
            nc.scalar.copy(out=kT[:, g, :], in_=kt_ps[:].rearrange("p t k -> p (t k)"))

        def transpose_q(m):
            h, g = divmod(m, NKV)
            qt_ps = psum.tile([P, REP, 2, P], BF16, tag="bank")
            for a in range(REP):
                for j in range(2):
                    nc.tensor.transpose(qt_ps[:, a, j, :], q_sb[:, h, g * REP + a, j, :], ident_bf[:])
            live["qT", m] = qt_ps

        def copy_qT(m):
            tiles = live["qT", m][:].rearrange("p a j (i w) -> p i (a j) w", i=2)
            for i in range(2):
                nc.scalar.copy(out=qT[:, m, i].rearrange("p a (j w) -> p (a j) w", j=2), in_=tiles[:, i])

        def group_vp():
            live["vp"] = work.tile([P, N_TILE * 4], BF16, align_bytes=64, bufs=1, name="v_grouped")
            nc.vector.tensor_copy(
                out=live["vp"][:].rearrange("p (g d t) -> p g d t", g=NKV, t=4),
                in_=vp_sb[:].rearrange("p g t d -> p g d t"),
            )

        def group_v(g):
            if g == 0:
                live["v"] = work.tile([P, N_TILE * 4], BF16, align_bytes=64, bufs=1, name="v_grouped")
            nc.gpsimd.tensor_scalar(
                out=live["v"][:].rearrange("p (g d t) -> p g d t", g=NKV, t=4)[:, g],
                in0=v_sb[:, g].rearrange("p t d -> p d t"),
                scalar1=1.0,
                scalar2=0.0,
                op0=ALU.mult,
                op1=ALU.add,
            )

        def quantise_v(v_grouped, codes, scales):
            nc.vector.quantize_mx(out=codes[:].bitcast(FP8X4), scales=scales[:], in_=v_grouped[:])

        def spread_v_pair():
            for c in range(2):
                rows = slice(64 * c, 64 * (c + 1))
                nc.vector.tensor_copy(
                    out=vp_codes[rows].bitcast(I32).rearrange("p (g c d) -> p g c d", g=NKV, c=2)[:, :, c],
                    in_=vd_codes[rows].bitcast(I32).rearrange("p (g d) -> p g d", g=NKV),
                )
                nc.vector.tensor_copy(
                    out=vp_scales[:].rearrange("p (g c d) -> p g c d", g=NKV, c=2)[:, :, c],
                    in_=vd_scales[:].rearrange("p (g d) -> p g d", g=NKV),
                )

        def scores(k):
            if not opens_bank(k):
                return
            n, a0 = divmod(k, REP)
            i, g = divmod(n, NKV)
            width = (i + 1) * P
            queries = qT[:, (i // 2) * NKV + g, i % 2]
            s_ps = psum.tile([P, BANK], F32, tag="bank")
            live["s", k] = s_ps
            for c in range(heads_per_bank(n)):
                lo = c * width
                diag = lo + i * P
                if i > 0:
                    nc.tensor.matmul(
                        out=s_ps[:, lo:diag], lhsT=queries[:, a0 + c, :], rhs=kT[:, g, 0 : i * P], start=True, stop=True
                    )
                nc.tensor.matmul(
                    out=s_ps[:, diag : diag + P], lhsT=order_rows[:], rhs=mask_bf[:], start=True, stop=False
                )
                nc.tensor.matmul(
                    out=s_ps[:, diag : diag + P],
                    lhsT=queries[:, a0 + c, :],
                    rhs=kT[:, g, i * P : (i + 1) * P],
                    start=False,
                    stop=True,
                )

        def row_max(k):
            if not opens_bank(k):
                return
            n, a0 = divmod(k, REP)
            width = (n // NKV + 1) * P
            count = heads_per_bank(n)
            if a0 == 0:
                live["max", n] = stat.tile([P, REP], F32, name="row_max")
                live["neg", n] = stat.tile([P, REP], F32, name="neg_max")
                live["sum", n] = stat.tile([P, REP], F32, name="row_sum")
            nc.vector.tensor_reduce(
                out=live["max", n][:, a0 : a0 + count],
                in_=live["s", k][:, 0 : count * width].rearrange("p (c w) -> p c w", c=count),
                axis=AXIS.X,
                op=ALU.max,
            )
            nc.gpsimd.tensor_scalar(
                out=live["neg", n][:, a0 : a0 + count],
                in0=live["max", n][:, a0 : a0 + count],
                scalar1=-SCALE,
                scalar2=0.0,
                op0=ALU.mult,
                op1=ALU.add,
            )

        def exp_head(k):
            if not 0 <= k < BEATS:
                return
            n, a = divmod(k, REP)
            width = (n // NKV + 1) * P
            c = a % heads_per_bank(n)
            if n < NARROW:
                pair = e_pair[(n % 2) * 2 + a // 2][:].rearrange("p (u c w e) -> p u c w e", u=2, c=2, e=2)
                e_out = pair[:, :, a % 2, 0 : width // 4, :]
            else:
                e_tile = e_wide[(n % 2) * REP + a]
                e_out = e_tile[:].rearrange("p (u w e) -> p u w e", u=2, e=2)[:, :, 0 : width // 4, :]
            nc.scalar.activation(
                out=e_out,
                in_=live["s", k - c][:, c * width : (c + 1) * width].rearrange("p (w u e) -> p u w e", u=2, e=2),
                func=ACT.Exp,
                bias=live["neg", n][:, a : a + 1],
                scale=SCALE,
                accum_out=live["sum", n][:, a : a + 1],
            )

        def reciprocal(n):
            if is_unit(n):
                live["inv", n] = stat.tile([P, REP], F32, name="inv_sum")
                nc.vector.reciprocal(out=live["inv", n][:], in_=live["sum", n][:])

        def transpose_e(n):
            if not is_unit(n):
                return
            tiles = e_pair[(n % 2) * 2 : (n % 2) * 2 + 2] if n < NARROW else e_wide[(n % 2) * REP : (n % 2 + 1) * REP]
            for half in range(len(tiles) // 2):
                et_ps = psum.tile([P, 2, 2, P], F32, tag="bank")
                live["eT", n, half] = et_ps
                for c in range(2):
                    e_words = tiles[2 * half + c][:].bitcast(F32)
                    for u in range(2):
                        nc.tensor.transpose(et_ps[:, c, u, :], e_words[:, u * P : (u + 1) * P], ident_f32[:])

        def copy_eT(n):
            if not is_unit(n):
                return
            e_grouped = work.tile([P, REP * P * 4], BF16, align_bytes=64)
            live["e_grouped", n] = e_grouped
            words = e_grouped[:].bitcast(F32).rearrange("p (a q u) -> p a q u", a=REP, u=2)
            nc.scalar.copy(out=words[:, 0:2], in_=live["eT", n, 0][:].rearrange("p c u q -> p c q u"))
            if n >= NARROW:
                copy = nc.scalar.copy if n % 2 else nc.vector.tensor_copy
                copy(out=words[:, 2:4], in_=live["eT", n, 1][:].rearrange("p c u q -> p c q u"))

        def quantise_e(n):
            if not is_unit(n):
                return
            e_codes = work.tile([P, REP * P], U32, align_bytes=256)
            e_scales = work.tile([P, REP * P], U8, align_bytes=256)
            live["e_codes", n] = e_codes
            live["e_scales", n] = e_scales
            count = (2 if n < NARROW else REP) * P
            nc.vector.quantize_mx(
                out=e_codes[:, 0:count].bitcast(FP8X4),
                scales=e_scales[:, 0:count],
                in_=live["e_grouped", n][:, 0 : 4 * count],
            )

        def e_times_v(n):
            if not is_unit(n):
                return
            g = n % NKV
            o_ps = psum.tile([P, REP * HD], F32, tag="bank")
            live["o", n] = o_ps
            codes, scales, width = (vp_codes, vp_scales, 2 * HD) if n < NARROW else (v_codes, v_scales, HD)
            for m in range(REP * HD // width):
                nc.tensor.matmul_mx(
                    out=o_ps[:, m * width : (m + 1) * width],
                    lhsT=live["e_codes", n][:, m * P : (m + 1) * P].bitcast(FP8X4),
                    lhsT_scale=live["e_scales", n][:, m * P : (m + 1) * P],
                    rhs=codes[:, g * width : (g + 1) * width].bitcast(FP8X4),
                    rhs_scale=scales[:, g * width : (g + 1) * width],
                    start=True,
                    stop=True,
                )

        def scale_o(n):
            if not is_unit(n):
                return
            o_sb = work.tile([P, REP * HD], BF16)
            live["o_sb", n] = o_sb
            nc.vector.tensor_tensor(
                out=o_sb[:].rearrange("p (a d) -> p a d", a=REP),
                in0=live["o", n][:].rearrange("p (a d) -> p a d", a=REP),
                in1=live["inv", n][:].unsqueeze(2).to_broadcast([P, REP, HD]),
                op=ALU.mult,
            )

        def transpose_o(n):
            if not is_unit(n):
                return
            o_words = live["o_sb", n][:].bitcast(F32)
            ot_ps = psum.tile([P, 2, P], F32, tag="bank")
            live["oT", n] = ot_ps
            for u in range(2):
                nc.tensor.transpose(ot_ps[:, u, :], o_words[:, u * P : (u + 1) * P], order_queries[:])

        def copy_oT(n):
            if not is_unit(n):
                return
            o_grouped = work.tile([P, P * 4], BF16, align_bytes=64)
            live["o_grouped", n] = o_grouped
            nc.scalar.copy(
                out=o_grouped[:].bitcast(F32).rearrange("p (q u) -> p q u", u=2),
                in_=live["oT", n][:].rearrange("p u q -> p q u"),
            )

        def quantise_o(n):
            if is_unit(n):
                nc.vector.quantize_mx(
                    out=o_codes[:, n, :].bitcast(FP8X4), scales=o_scales[:, n, :], in_=live["o_grouped", n][:]
                )

        def transpose_wo(f):
            if not 0 <= f < WO_BANKS:
                return
            c, g = divmod(f, PASSES)
            wt_ps = psum.tile([P, 2, 2, P], F32, tag="bank")
            live["wT", f] = wt_ps
            for b in range(2):
                w_words = wo_sb[:, 2 * c + b, :].bitcast(F32)
                for u in range(2):
                    first = g * (K_PASS // 2) + u * P
                    nc.tensor.transpose(wt_ps[:, b, u, :], w_words[:, first : first + P], ident_f32[:])

        def copy_woT(f):
            if not 0 <= f < WO_BANKS:
                return
            w_grouped = work.tile([P, WO_ROWS * 4], BF16, align_bytes=64, bufs=5)
            live["w_grouped", f] = w_grouped
            words = w_grouped[:].bitcast(F32).rearrange("p (b n u) -> p b n u", b=2, u=2)
            source = live["wT", f][:].rearrange("p b u n -> p b n u")
            if f % 4 == 0:
                nc.vector.tensor_copy(out=words, in_=source)
            else:
                nc.scalar.copy(out=words, in_=source)

        def quantise_wo(f):
            if not 0 <= f < WO_BANKS:
                return
            c, g = divmod(f, PASSES)
            cols = slice(c * WO_ROWS, (c + 1) * WO_ROWS)
            nc.vector.quantize_mx(
                out=w_codes[:, g, cols].bitcast(FP8X4), scales=w_scales[:, g, cols], in_=live["w_grouped", f][:]
            )

        def project_pass(acc, i, nt, g):
            cols = slice(nt * N_TILE, (nt + 1) * N_TILE)
            nc.tensor.matmul_mx(
                out=acc[:],
                lhsT=o_codes[:, i * NKV + g, :].bitcast(FP8X4),
                lhsT_scale=o_scales[:, i * NKV + g, :],
                rhs=w_codes[:, g, cols].bitcast(FP8X4),
                rhs_scale=w_scales[:, g, cols],
                start=(g == 0),
                stop=(g == PASSES - 1),
            )

        def store(acc, i, nt, engine_copy):
            out_sb = work.tile([P, N_TILE], F32, bufs=5)
            engine_copy(out=out_sb[:], in_=acc[:])
            nc.sync.dma_start(out=out[0, i * P : (i + 1) * P, nt * N_TILE : (nt + 1) * N_TILE], in_=out_sb[:])

        def project(job):
            i, nt = divmod(job, NT)
            f_ps = psum.tile([P, N_TILE], F32, tag="bank")
            live["f", job] = f_ps
            for g in range(PASSES):
                project_pass(f_ps, i, nt, g)

        def wo_upto(beat):
            return min(WO_BANKS, sum(WO_PER_BEAT[b % REP] for b in range(WO_FIRST_BEAT, beat + 1)))

        def wo_banks(beat):
            return range(wo_upto(beat - 1), wo_upto(beat))

        def project_beats():
            beats = {}
            beat = 0
            for job in range(3 * NT):
                i, nt = divmod(job, NT)
                o_ready = REP * (NKV * i + NKV - 1) + QUANTISE_O + 1
                step = 2 if i == 2 and nt > 0 else REP
                while (
                    beat % step != 2 % step
                    or beat < o_ready
                    or wo_upto(beat - 1 - QUANTISE_WO) < (WO_BANKS // NT) * (nt + 1)
                ):
                    beat += 1
                beats[beat] = job
                beat += 1
            return beats

        def project_last(g):
            for nt in range(NT):
                project_pass(last[nt], QT - 1, nt, g)

        jobs = project_beats()
        last_passes = {66: 0, 68: 1, 71: 2}
        last = []

        def due(beat, delay):
            n, rest = divmod(beat - delay, REP)
            return n if rest == 0 and is_unit(n) else -1

        def q_beat(m):
            h, g = divmod(m, NKV)
            return SECOND_Q + REP * g if h else max(REP * g + TRANSPOSE_Q, -SCORES_AHEAD)

        transpose_k(0)
        transpose_q(0)
        copy_qT(0)
        for beat in range(-SCORES_AHEAD, REP * (UNITS - 1) + QUANTISE_O + 1):
            quantise_o(due(beat, QUANTISE_O))
            copy_oT(due(beat, COPY_O))
            scale_o(due(beat, SCALE_O))
            e_times_v(due(beat, TIMES_V))
            quantise_e(due(beat, QUANTISE_E))
            copy_eT(due(beat, COPY_E))
            transpose_e(due(beat, TRANSPOSE_E))
            for f in wo_banks(beat - QUANTISE_WO):
                quantise_wo(f)
            exp_head(beat)
            scores(beat + SCORES_AHEAD)
            transpose_o(due(beat, TRANSPOSE_O))
            row_max(beat + MAX_AHEAD)
            reciprocal(due(beat, COPY_E))
            for m in range(1, 2 * NKV):
                if beat == q_beat(m) + 1:
                    copy_qT(m)
                if beat == q_beat(m):
                    if m < NKV:
                        transpose_k(m)
                    transpose_q(m)
            if beat - 1 in jobs:
                job = jobs[beat - 1]
                store(live["f", job], job // NT, job % NT, nc.scalar.copy)
            for f in wo_banks(beat - COPY_WO):
                copy_woT(f)
            for f in wo_banks(beat):
                transpose_wo(f)
            if beat == PREPARE_VP:
                group_vp()
            if beat == PREPARE_VP + 1:
                quantise_v(live["vp"], vd_codes, vd_scales)
            if beat == PREPARE_VP + 2:
                spread_v_pair()
            if 0 <= beat - PREPARE_V < NKV:
                group_v(beat - PREPARE_V)
            if beat == PREPARE_V + 6:
                quantise_v(live["v"], v_codes, v_scales)
            if beat in jobs:
                project(jobs[beat])
            if beat in last_passes:
                if not last:
                    last.extend(psum.tile([P, N_TILE], F32, tag="bank", name="last%d" % nt) for nt in range(NT))
                project_last(last_passes[beat])
        project_last(PASSES - 1)
        for nt in range(NT):
            store(last[nt], QT - 1, nt, nc.vector.tensor_copy if nt % 2 else nc.scalar.copy)
